import numpy as np
import ml_dtypes


def mxq(x, axis, fmt="e4m3"):
    dtype, down = {"e4m3": (ml_dtypes.float8_e4m3fn, 7), "e5m2": (ml_dtypes.float8_e5m2, 14)}[fmt]
    v = np.moveaxis(np.asarray(x, np.float32).astype(ml_dtypes.bfloat16).astype(np.float64), axis, -1)
    blocks = v.reshape(v.shape[:-1] + (-1, 32))
    amax = np.abs(blocks).max(-1, keepdims=True)
    byte = np.maximum(np.where(amax > 0, np.frexp(amax)[1] - 1 + 127, 0) - down, 1)
    scale = np.exp2(byte - 127.0)
    codes = (blocks / scale).astype(np.float32).astype(dtype).astype(np.float64)
    return np.moveaxis((codes * scale).reshape(v.shape), -1, axis)


WIDE = False


def mx_kscale(k):
    if not WIDE:
        return np.ones(k)
    levels = np.array([10, -10, 5, -5, 0])
    a = np.random.permutation(np.resize(levels, k // 512 * 4)).reshape(k // 512, 4)
    idx = np.arange(k)
    return np.exp2(a[idx // 512, idx % 128 // 32])


BF16 = ml_dtypes.bfloat16


def bf(x):
    return np.asarray(x, np.float32).astype(BF16)


def f64(x):
    return np.asarray(x).astype(np.float64)


B, S, H, D, M = 2, 2048, 2, 512, 512
E = H * D
R = B * S
EPS = 1e-6
QK = np.sqrt(1.5) / D ** 0.25


def setup_inputs():
    s = mx_kscale(M)
    q = np.random.standard_normal((B, S, H, D)) * QK
    k = np.random.standard_normal((H, M, D)) * QK
    q[..., 0] = np.log(2.0)
    k[:, :, 0] += np.log2(s)[None, :]
    v = np.random.standard_normal((H, M, D)) / s[None, :, None] * np.mean(s)
    return {"q_scaled": bf(q),
            "k": bf(k),
            "v": bf(v),
            "norm_retrieved_w": bf(1.0 + 0.1 * np.random.standard_normal(E)),
            "query_input": bf(np.random.standard_normal((B, S, E)))}


def reference(q_scaled, k, v, norm_retrieved_w, query_input):
    q = f64(q_scaled).reshape(R, H, D)
    kk = f64(k)
    vv = f64(v)
    heads = []
    for h in range(H):
        s = q[:, h, :] @ kk[h].T
        e = np.exp(s - s.max(1, keepdims=True))
        heads.append((mxq(e, 1, "e4m3") @ mxq(vv[h], 0, "e4m3")) / e.sum(1, keepdims=True))
    attn_flat = np.concatenate(heads, 1)
    retrieved = attn_flat * (1.0 / np.sqrt(np.mean(attn_flat * attn_flat, 1, keepdims=True) + EPS)) * f64(norm_retrieved_w)
    return (retrieved + f64(query_input).reshape(R, E)).reshape(B, S, E)

@@ -1,0 +1,288 @@
+from contextlib import ExitStack
+
+import concourse.bass as bass
+import concourse.mybir as mybir
+import concourse.tile as tile
+from concourse.masks import make_identity
+
+F32 = mybir.dt.float32
+BF16 = mybir.dt.bfloat16
+U32 = mybir.dt.uint32
+U8 = mybir.dt.uint8
+FP8X4 = mybir.dt.float8_e4m3fn_x4
+ACT = mybir.ActivationFunctionType
+ALU = mybir.AluOpType
+AX = mybir.AxisListType
+
+P = 128
+H = 2
+D = 512
+M = 512
+E = H * D
+R = 4096
+TPC = 4
+NCH = R // (P * TPC)
+NT = R // P
+EPS = 1e-6
+FLOPS = 2 * R * M * D * H * 2
+
+E_WORDS = True
+PIN = True
+
+
+def tile_hopfieldmemorylayer_pb_t_kernel(tc, q_scaled, k, v, norm_retrieved_w, query_input, out):
+    nc = tc.nc
+    qv = q_scaled.rearrange("b s h d -> (b s) (h d)").rearrange("(c p t) e -> c p t e", p=P, t=TPC)
+    xv = query_input.rearrange("b s e -> (b s) e").rearrange("(c p t) e -> c p t e", p=P, t=TPC)
+    ov = out.rearrange("b s e -> (b s) e").rearrange("(c p t) e -> c p t e", p=P, t=TPC)
+
+    with ExitStack() as ctx:
+        const = ctx.enter_context(tc.tile_pool(name="const", bufs=1))
+        work = ctx.enter_context(tc.tile_pool(name="work", bufs=2))
+        small = ctx.enter_context(tc.tile_pool(name="small", bufs=6))
+        psum = ctx.enter_context(tc.psum_pool(name="psum", bufs=1))
+        if PIN:
+            ctx.enter_context(tc.manual_schedule())
+
+        ident = const.tile([P, P], F32, name="ident")
+        make_identity(nc, ident[:])
+        if not E_WORDS:
+            ident_bf = const.tile([P, P], BF16, name="ident_bf")
+            make_identity(nc, ident_bf[:])
+        mhalf = const.tile([P, 1], F32, name="mhalf")
+        nc.vector.memset(mhalf[:], -0.5)
+        warm = const.tile([P, 1], F32, name="warm")
+        nc.scalar.activation(out=warm[:], in_=mhalf[:], func=ACT.Exp)
+
+        k_sb = [const.tile([P, 4, D], BF16, name="k_sb%d" % h) for h in range(H)]
+        v_raw = [const.tile([P, 4, D], BF16, name="v_raw%d" % h) for h in range(H)]
+        q_sb = [const.tile([P, TPC, E], BF16, name="q_sb%d" % c) for c in range(NCH)]
+        x_sb = [const.tile([P, TPC, E], BF16, name="x_sb%d" % c) for c in range(NCH)]
+        w_bc = const.tile([P, E], BF16, name="w_bc")
+        nc.sync.dma_start(out=k_sb[0][:], in_=k[0].rearrange("(a p) d -> p a d", p=P))
+        nc.sync.dma_start(out=q_sb[0][:, 0:1, :], in_=qv[0][:, 0:1, :])
+        nc.sync.dma_start(out=k_sb[1][:], in_=k[1].rearrange("(a p) d -> p a d", p=P))
+        nc.sync.dma_start(out=q_sb[0][:, 1:TPC, :], in_=qv[0][:, 1:TPC, :])
+        for h in range(H):
+            nc.sync.dma_start(out=v_raw[h][:], in_=v[h].rearrange("(p j) w -> p j w", j=4))
+        nc.sync.dma_start(out=w_bc[:], in_=norm_retrieved_w.partition_broadcast(P))
+        nc.sync.dma_start(out=x_sb[0][:], in_=xv[0])
+        for c in range(1, NCH):
+            nc.sync.dma_start(out=q_sb[c][:], in_=qv[c])
+            nc.sync.dma_start(out=x_sb[c][:], in_=xv[c])
+
+        kT = [const.tile([P, 2, 2, M], BF16, name="kT%d" % h) for h in range(H)]
+        for h in range(H):
+            for g in range(2):
+                pk = psum.tile([P, M], F32, name="pk", tag="acc", bufs=4)
+                for a in range(4):
+                    nc.tensor.transpose(pk[:, a * P:(a + 1) * P], k_sb[h][:, a, :].bitcast(F32)[:, g * P:(g + 1) * P], ident[:])
+                for eps in range(2):
+                    if E_WORDS:
+                        src = pk[:].bitcast(BF16).rearrange("q (p u f s) -> q s u p f", u=2, f=2, s=2)[:, eps]
+                        dst = kT[h][:, g, eps, :].rearrange("q (u p f) -> q u p f", u=2, f=2)
+                    else:
+                        src = pk[:].bitcast(BF16).rearrange("q (p t s) -> q s t p", t=4, s=2)[:, eps]
+                        dst = kT[h][:, g, eps, :].rearrange("q (t p) -> q t p", t=4)
+                    if eps == 0:
+                        nc.vector.tensor_copy(out=dst, in_=src)
+                    else:
+                        nc.scalar.copy(out=dst, in_=src)
+
+        v_codes = [const.tile([P, D], U32, name="v_codes%d" % h, align_bytes=64) for h in range(H)]
+        v_scales = [const.tile([P, D], U8, name="v_scales%d" % h, align_bytes=64) for h in range(H)]
+        v_grp = [const.tile([P, D, 4], BF16, name="v_grp%d" % h, align_bytes=64) for h in range(H)]
+
+        def v_regroup(h):
+            nc.vector.tensor_copy(out=v_grp[h][:], in_=v_raw[h][:].rearrange("p j w -> p w j"))
+
+        def v_quant(h):
+            nc.vector.quantize_mx(out=v_codes[h][:].bitcast(FP8X4), scales=v_scales[h][:],
+                                  in_=v_grp[h][:].rearrange("p w j -> p (w j)"))
+
+        st = {}
+
+        def ok(i):
+            return 0 <= i < NT
+
+        def tq(i, bs):
+            if not ok(i):
+                return
+            c, t = divmod(i, TPC)
+            if ("ptq", i) not in st:
+                st[("ptq", i)] = psum.tile([P, 4 * P], F32, name="ptq", tag="tq", bufs=1)
+            for b in bs:
+                nc.tensor.transpose(st[("ptq", i)][:, b * P:(b + 1) * P], q_sb[c][:, t, :].bitcast(F32)[:, b * P:(b + 1) * P], ident[:])
+
+        def copy_q(i):
+            if not ok(i):
+                return
+            st[("qT", i)] = work.tile([P, 4 * P], F32, name="qT", tag="qT", bufs=3)
+            nc.scalar.copy(out=st[("qT", i)][:], in_=st[("ptq", i)][:])
+
+        def mm(i, h, js):
+            if not ok(i):
+                return
+            if ("s", i, h) not in st:
+                st[("s", i, h)] = psum.tile([P, M], F32, name="ps_s", tag="s", bufs=2)
+            qb = st[("qT", i)][:].bitcast(BF16).rearrange("p (b r s) -> p b r s", b=4, s=2)
+            for j in js:
+                g, eps = divmod(j, 2)
+                nc.tensor.matmul(out=st[("s", i, h)][:], lhsT=qb[:, 2 * h + g, :, eps], rhs=kT[h][:, g, eps, :],
+                                 start=(j == 0), stop=(j == 3))
+
+        def negmax(i, h):
+            if not ok(i):
+                return
+            if h == 0:
+                st[("nm", i)] = small.tile([P, H], F32, name="nm", tag="nm")
+            nc.vector.tensor_reduce(out=st[("nm", i)][:, h:h + 1], in_=st[("s", i, h)][:], axis=AX.X, op=ALU.max, negate=True)
+
+        def expo(i, h):
+            if not ok(i):
+                return
+            if h == 0:
+                st[("e", i)] = work.tile([P, H, M], BF16, name="e_sb", tag="e", bufs=3)
+                st[("rs", i)] = small.tile([P, H], F32, name="rs", tag="rs")
+            nc.scalar.activation(out=st[("e", i)][:, h, :], in_=st[("s", i, h)][:], func=ACT.Exp,
+                                 bias=st[("nm", i)][:, h:h + 1], scale=1.0, accum_out=st[("rs", i)][:, h:h + 1])
+
+        def recip(i):
+            if not ok(i):
+                return
+            st[("inv", i)] = small.tile([P, H], F32, name="inv", tag="inv")
+            nc.vector.reciprocal(out=st[("inv", i)][:], in_=st[("rs", i)][:])
+
+        def te(i, h, us):
+            if not ok(i):
+                return
+            if ("pte", i) not in st:
+                if E_WORDS:
+                    st[("pte", i)] = psum.tile([P, H, 2, P], F32, name="pte", tag="te", bufs=1)
+                else:
+                    st[("pte", i)] = psum.tile([P, H, 4, P], BF16, name="pte", tag="te", bufs=1)
+            for u in us:
+                if E_WORDS:
+                    nc.tensor.transpose(st[("pte", i)][:, h, u, :], st[("e", i)][:, h, :].bitcast(F32)[:, u * P:(u + 1) * P], ident[:])
+                else:
+                    nc.tensor.transpose(st[("pte", i)][:, h, u, :], st[("e", i)][:, h, u * P:(u + 1) * P], ident_bf[:])
+
+        def copy_e(i):
+            if not ok(i):
+                return
+            if E_WORDS:
+                st[("gq", i)] = work.tile([P, H, P, 2], F32, name="gq", tag="gq", bufs=2, align_bytes=64)
+            else:
+                st[("gq", i)] = work.tile([P, H, P, 4], BF16, name="gq", tag="gq", bufs=2, align_bytes=64)
+            nc.vector.tensor_copy(out=st[("gq", i)][:], in_=st[("pte", i)][:].rearrange("p h u r -> p h r u"))
+
+        def quant(i):
+            if not ok(i):
+                return
+            st[("cd", i)] = work.tile([P, H * P], U32, name="cd", tag="cd", bufs=2, align_bytes=64)
+            st[("sc", i)] = work.tile([P, H * P], U8, name="sc", tag="sc", bufs=2, align_bytes=64)
+            flat = st[("gq", i)][:].rearrange("p h r u -> p (h r u)")
+            if E_WORDS:
+                flat = flat.bitcast(BF16)
+            nc.vector.quantize_mx(out=st[("cd", i)][:].bitcast(FP8X4), scales=st[("sc", i)][:], in_=flat)
+
+        def mx(i):
+            if not ok(i):
+                return
+            for h in range(H):
+                st[("acc", i, h)] = psum.tile([P, D], F32, name="acc", tag="acc", bufs=4)
+                nc.tensor.matmul_mx(out=st[("acc", i, h)][:],
+                                    lhsT=st[("cd", i)][:, h * P:(h + 1) * P].bitcast(FP8X4),
+                                    lhsT_scale=st[("sc", i)][:, h * P:(h + 1) * P],
+                                    rhs=v_codes[h][:].bitcast(FP8X4), rhs_scale=v_scales[h][:],
+                                    start=True, stop=True)
+
+        def sq(i, h):
+            if not ok(i):
+                return
+            if h == 0:
+                st[("ss", i)] = small.tile([P, H], F32, name="ss", tag="ss")
+            junk = work.tile([P, D], BF16, name="junk", tag="junk", bufs=2)
+            nc.scalar.activation(out=junk[:], in_=st[("acc", i, h)][:], func=ACT.Square,
+                                 scale=st[("inv", i)][:, h:h + 1], accum_out=st[("ss", i)][:, h:h + 1])
+
+        def chain(i):
+            if not ok(i):
+                return
+            z = small.tile([P, 1], F32, name="z", tag="z")
+            rr = small.tile([P, 1], F32, name="rr", tag="rr")
+            st[("c", i)] = small.tile([P, H], F32, name="cc", tag="cc")
+            nc.gpsimd.tensor_scalar(out=z[:], in0=st[("ss", i)][:, 0:1], scalar1=st[("ss", i)][:, 1:2], scalar2=E * EPS,
+                                    op0=ALU.add, op1=ALU.add)
+            nc.gpsimd.tensor_tensor(out=rr[:], in0=z[:], in1=mhalf[:], op=ALU.pow)
+            nc.gpsimd.tensor_scalar(out=st[("c", i)][:], in0=st[("inv", i)][:], scalar1=rr[:, 0:1], scalar2=32.0,
+                                    op0=ALU.mult, op1=ALU.mult)
+
+        def stt(i, h):
+            if not ok(i):
+                return
+            if h == 0:
+                st[("o", i)] = work.tile([P, E], F32, name="o_sb", tag="o", bufs=4)
+            nc.vector.scalar_tensor_tensor(out=st[("o", i)][:, h * D:(h + 1) * D], in0=st[("acc", i, h)][:],
+                                           scalar=st[("c", i)][:, h:h + 1], in1=w_bc[:, h * D:(h + 1) * D],
+                                           op0=ALU.mult, op1=ALU.mult)
+
+        def addx(i, h):
+            if not ok(i):
+                return
+            c, t = divmod(i, TPC)
+            o = st[("o", i)][:, h * D:(h + 1) * D]
+            nc.gpsimd.tensor_tensor(out=o, in0=o, in1=x_sb[c][:, t, h * D:(h + 1) * D], op=ALU.add)
+
+        def store(i):
+            if not ok(i):
+                return
+            c, t = divmod(i, TPC)
+            nc.sync.dma_start(out=ov[c][:, t, :], in_=st[("o", i)][:])
+
+        for i in range(-1, NT + 3):
+            copy_e(i - 2)
+            expo(i - 1, 1)
+            mm(i, 0, [0])
+            tq(i + 1, [0, 1])
+            mm(i, 0, [1])
+            tq(i + 1, [2, 3])
+            mm(i, 0, [2])
+            if not E_WORDS:
+                te(i - 1, 0, [0, 1])
+            mm(i, 0, [3])
+            if not E_WORDS:
+                te(i - 1, 0, [2, 3])
+            copy_q(i + 1)
+            negmax(i, 0)
+            expo(i, 0)
+            quant(i - 2)
+            recip(i - 1)
+            if i == 0:
+                v_regroup(0)
+                v_regroup(1)
+            if i == 1:
+                v_quant(0)
+                v_quant(1)
+            mm(i, 1, [0])
+            if E_WORDS:
+                te(i - 1, 0, [0, 1])
+            else:
+                te(i - 1, 1, [0, 1])
+            mm(i, 1, [1])
+            if E_WORDS:
+                te(i - 1, 1, [0, 1])
+            else:
+                te(i - 1, 1, [2, 3])
+            mm(i, 1, [2])
+            mx(i - 2)
+            mm(i, 1, [3])
+            stt(i - 3, 0)
+            addx(i - 3, 0)
+            stt(i - 3, 1)
+            sq(i - 2, 0)
+            sq(i - 2, 1)
+            chain(i - 2)
+            addx(i - 3, 1)
+            store(i - 3)
+            negmax(i, 1)

@@ -27,6 +27,40 @@ EPS = 1e-6
 FLOPS = 2 * R * M * D * H * 2
 
 E_WORDS = True
+CE_V_EVERY = 4
+ADD0_G_EVERY = 0
+SCHED = [
+    ("mm", 0, (0, 0), None),
+    ("copy_e", 2, None, "alt"),
+    ("tq", -1, (0, 1), None),
+    ("add", 5, 0, "V"),
+    ("mm", 0, (0, 1), None),
+    ("tq", -1, (2, 3), None),
+    ("mm", 0, (0, 2), None),
+    ("exp", 1, 1, None),
+    ("copy_q", -1, None, None),
+    ("quant", 2, None, None),
+    ("mm", 0, (0, 3), None),
+    ("mx", 3, 0, None),
+    ("negmax", 0, 0, None),
+    ("mx", 3, 1, None),
+    ("add", 5, 1, "G"),
+    ("store", 5, None, None),
+    ("mm", 0, (1, 0), None),
+    ("sq", 3, 0, None),
+    ("te", 1, 0, None),
+    ("mm", 0, (1, 1), None),
+    ("exp", 0, 0, None),
+    ("te", 1, 1, None),
+    ("mm", 0, (1, 2), None),
+    ("sq", 3, 1, None),
+    ("chain", 3, None, None),
+    ("mm", 0, (1, 3), None),
+    ("recip", 2, None, None),
+    ("stt", 4, 1, None),
+    ("stt", 4, 0, None),
+    ("negmax", 0, 1, None),
+]
 PIN = True
 
 
@@ -39,7 +73,7 @@ def tile_hopfieldmemorylayer_pb_t_kernel(tc, q_scaled, k, v, norm_retrieved_w, q
     with ExitStack() as ctx:
         const = ctx.enter_context(tc.tile_pool(name="const", bufs=1))
         work = ctx.enter_context(tc.tile_pool(name="work", bufs=2))
-        small = ctx.enter_context(tc.tile_pool(name="small", bufs=6))
+        small = ctx.enter_context(tc.tile_pool(name="small", bufs=8))
         psum = ctx.enter_context(tc.psum_pool(name="psum", bufs=1))
         if PIN:
             ctx.enter_context(tc.manual_schedule())
@@ -167,29 +201,32 @@ def tile_hopfieldmemorylayer_pb_t_kernel(tc, q_scaled, k, v, norm_retrieved_w, q
                 else:
                     nc.tensor.transpose(st[("pte", i)][:, h, u, :], st[("e", i)][:, h, u * P:(u + 1) * P], ident_bf[:])
 
-        def copy_e(i):
+        def copy_e(i, eng):
             if not ok(i):
                 return
             if E_WORDS:
                 st[("gq", i)] = work.tile([P, H, P, 2], F32, name="gq", tag="gq", bufs=2, align_bytes=64)
             else:
                 st[("gq", i)] = work.tile([P, H, P, 4], BF16, name="gq", tag="gq", bufs=2, align_bytes=64)
-            nc.vector.tensor_copy(out=st[("gq", i)][:], in_=st[("pte", i)][:].rearrange("p h u r -> p h r u"))
+            if eng == "V":
+                nc.vector.tensor_copy(out=st[("gq", i)][:], in_=st[("pte", i)][:].rearrange("p h u r -> p h r u"))
+            else:
+                nc.scalar.copy(out=st[("gq", i)][:], in_=st[("pte", i)][:].rearrange("p h u r -> p h r u"))
 
         def quant(i):
             if not ok(i):
                 return
-            st[("cd", i)] = work.tile([P, H * P], U32, name="cd", tag="cd", bufs=2, align_bytes=64)
-            st[("sc", i)] = work.tile([P, H * P], U8, name="sc", tag="sc", bufs=2, align_bytes=64)
+            st[("cd", i)] = work.tile([P, H * P], U32, name="cd", tag="cd", bufs=3, align_bytes=64)
+            st[("sc", i)] = work.tile([P, H * P], U8, name="sc", tag="sc", bufs=3, align_bytes=64)
             flat = st[("gq", i)][:].rearrange("p h r u -> p (h r u)")
             if E_WORDS:
                 flat = flat.bitcast(BF16)
             nc.vector.quantize_mx(out=st[("cd", i)][:].bitcast(FP8X4), scales=st[("sc", i)][:], in_=flat)
 
-        def mx(i):
+        def mx(i, hs):
             if not ok(i):
                 return
-            for h in range(H):
+            for h in hs:
                 st[("acc", i, h)] = psum.tile([P, D], F32, name="acc", tag="acc", bufs=4)
                 nc.tensor.matmul_mx(out=st[("acc", i, h)][:],
                                     lhsT=st[("cd", i)][:, h * P:(h + 1) * P].bitcast(FP8X4),
@@ -221,18 +258,21 @@ def tile_hopfieldmemorylayer_pb_t_kernel(tc, q_scaled, k, v, norm_retrieved_w, q
         def stt(i, h):
             if not ok(i):
                 return
-            if h == 0:
+            if ("o", i) not in st:
                 st[("o", i)] = work.tile([P, E], F32, name="o_sb", tag="o", bufs=4)
             nc.vector.scalar_tensor_tensor(out=st[("o", i)][:, h * D:(h + 1) * D], in0=st[("acc", i, h)][:],
                                            scalar=st[("c", i)][:, h:h + 1], in1=w_bc[:, h * D:(h + 1) * D],
                                            op0=ALU.mult, op1=ALU.mult)
 
-        def addx(i, h):
+        def addx(i, h, eng):
             if not ok(i):
                 return
             c, t = divmod(i, TPC)
             o = st[("o", i)][:, h * D:(h + 1) * D]
-            nc.gpsimd.tensor_tensor(out=o, in0=o, in1=x_sb[c][:, t, h * D:(h + 1) * D], op=ALU.add)
+            if eng == "V":
+                nc.vector.tensor_tensor(out=o, in0=o, in1=x_sb[c][:, t, h * D:(h + 1) * D], op=ALU.add)
+            else:
+                nc.gpsimd.tensor_tensor(out=o, in0=o, in1=x_sb[c][:, t, h * D:(h + 1) * D], op=ALU.add)
 
         def store(i):
             if not ok(i):
@@ -240,49 +280,47 @@ def tile_hopfieldmemorylayer_pb_t_kernel(tc, q_scaled, k, v, norm_retrieved_w, q
             c, t = divmod(i, TPC)
             nc.sync.dma_start(out=ov[c][:, t, :], in_=st[("o", i)][:])
 
-        for i in range(-1, NT + 3):
-            copy_e(i - 2)
-            expo(i - 1, 1)
-            mm(i, 0, [0])
-            tq(i + 1, [0, 1])
-            mm(i, 0, [1])
-            tq(i + 1, [2, 3])
-            mm(i, 0, [2])
-            if not E_WORDS:
-                te(i - 1, 0, [0, 1])
-            mm(i, 0, [3])
-            if not E_WORDS:
-                te(i - 1, 0, [2, 3])
-            copy_q(i + 1)
-            negmax(i, 0)
-            expo(i, 0)
-            quant(i - 2)
-            recip(i - 1)
-            if i == 0:
-                v_regroup(0)
-                v_regroup(1)
-            if i == 1:
-                v_quant(0)
-                v_quant(1)
-            mm(i, 1, [0])
-            if E_WORDS:
-                te(i - 1, 0, [0, 1])
-            else:
-                te(i - 1, 1, [0, 1])
-            mm(i, 1, [1])
-            if E_WORDS:
-                te(i - 1, 1, [0, 1])
-            else:
-                te(i - 1, 1, [2, 3])
-            mm(i, 1, [2])
-            mx(i - 2)
-            mm(i, 1, [3])
-            stt(i - 3, 0)
-            addx(i - 3, 0)
-            stt(i - 3, 1)
-            sq(i - 2, 0)
-            sq(i - 2, 1)
-            chain(i - 2)
-            addx(i - 3, 1)
-            store(i - 3)
-            negmax(i, 1)
+        for it in range(-3, NT + 9):
+            for name, lag, arg, eng in SCHED:
+                i = it - lag
+                if not ok(i):
+                    continue
+                if name == "mm":
+                    mm(i, arg[0], [arg[1]])
+                elif name == "tq":
+                    tq(i, arg)
+                elif name == "te":
+                    te(i, arg, [0, 1])
+                elif name == "mx":
+                    mx(i, [arg])
+                elif name == "copy_q":
+                    copy_q(i)
+                elif name == "copy_e":
+                    copy_e(i, "V" if i % CE_V_EVERY == CE_V_EVERY - 1 else "S")
+                elif name == "quant":
+                    quant(i)
+                elif name == "negmax":
+                    negmax(i, arg)
+                    if i == 0 and arg == 0:
+                        v_regroup(0)
+                        v_regroup(1)
+                    if i == 1 and arg == 0:
+                        v_quant(0)
+                        v_quant(1)
+                elif name == "exp":
+                    expo(i, arg)
+                elif name == "recip":
+                    recip(i)
+                elif name == "sq":
+                    sq(i, arg)
+                elif name == "chain":
+                    chain(i)
+                elif name == "stt":
+                    stt(i, arg)
+                elif name == "add":
+                    if arg == 0 and ADD0_G_EVERY > 0 and i % ADD0_G_EVERY == ADD0_G_EVERY - 1:
+                        addx(i, arg, "G")
+                    else:
+                        addx(i, arg, eng)
+                elif name == "store":
+                    store(i)

@@ -32,11 +32,12 @@ ADD0_G_EVERY = 0
 SCHED = [
     ("mm", 0, (0, 0), None),
     ("copy_e", 2, None, "alt"),
-    ("tq", -1, (0, 1), None),
+    ("tq", -1, (0, 1, 2), None),
     ("add", 5, 0, "V"),
     ("mm", 0, (0, 1), None),
-    ("tq", -1, (2, 3), None),
+    ("tq", -1, (3, 4, 5), None),
     ("mm", 0, (0, 2), None),
+    ("tq", -1, (6, 7), None),
     ("exp", 1, 1, None),
     ("copy_q", -1, None, None),
     ("quant", 2, None, None),
@@ -80,9 +81,8 @@ def tile_hopfieldmemorylayer_pb_t_kernel(tc, q_scaled, k, v, norm_retrieved_w, q
 
         ident = const.tile([P, P], F32, name="ident")
         make_identity(nc, ident[:])
-        if not E_WORDS:
-            ident_bf = const.tile([P, P], BF16, name="ident_bf")
-            make_identity(nc, ident_bf[:])
+        ident_bf = const.tile([P, P], BF16, name="ident_bf")
+        make_identity(nc, ident_bf[:])
         mhalf = const.tile([P, 1], F32, name="mhalf")
         nc.vector.memset(mhalf[:], -0.5)
         warm = const.tile([P, 1], F32, name="warm")
@@ -105,20 +105,18 @@ def tile_hopfieldmemorylayer_pb_t_kernel(tc, q_scaled, k, v, norm_retrieved_w, q
             nc.sync.dma_start(out=q_sb[c][:], in_=qv[c])
             nc.sync.dma_start(out=x_sb[c][:], in_=xv[c])
 
-        kT = [const.tile([P, 2, 2, M], BF16, name="kT%d" % h) for h in range(H)]
+        kT = [const.tile([P, 4, M], BF16, name="kT%d" % h) for h in range(H)]
         for h in range(H):
-            for g in range(2):
-                pk = psum.tile([P, M], F32, name="pk", tag="acc", bufs=4)
-                for a in range(4):
-                    nc.tensor.transpose(pk[:, a * P:(a + 1) * P], k_sb[h][:, a, :].bitcast(F32)[:, g * P:(g + 1) * P], ident[:])
-                for eps in range(2):
-                    if E_WORDS:
-                        src = pk[:].bitcast(BF16).rearrange("q (p u f s) -> q s u p f", u=2, f=2, s=2)[:, eps]
-                        dst = kT[h][:, g, eps, :].rearrange("q (u p f) -> q u p f", u=2, f=2)
-                    else:
-                        src = pk[:].bitcast(BF16).rearrange("q (p t s) -> q s t p", t=4, s=2)[:, eps]
-                        dst = kT[h][:, g, eps, :].rearrange("q (t p) -> q t p", t=4)
-                    if eps == 0:
+            for gp in range(2):
+                pk = psum.tile([P, 2, M], BF16, name="pk", tag="acc", bufs=4)
+                for g2 in range(2):
+                    g = 2 * gp + g2
+                    for a in range(4):
+                        nc.tensor.transpose(pk[:, g2, a * P:(a + 1) * P], k_sb[h][:, a, g * P:(g + 1) * P], ident_bf[:])
+                for g2 in range(2):
+                    src = pk[:, g2, :].rearrange("q (p u f) -> q u p f", u=2, f=2)
+                    dst = kT[h][:, 2 * gp + g2, :].rearrange("q (u p f) -> q u p f", u=2, f=2)
+                    if g2 == 0:
                         nc.vector.tensor_copy(out=dst, in_=src)
                     else:
                         nc.scalar.copy(out=dst, in_=src)
@@ -144,14 +142,14 @@ def tile_hopfieldmemorylayer_pb_t_kernel(tc, q_scaled, k, v, norm_retrieved_w, q
                 return
             c, t = divmod(i, TPC)
             if ("ptq", i) not in st:
-                st[("ptq", i)] = psum.tile([P, 4 * P], F32, name="ptq", tag="tq", bufs=1)
+                st[("ptq", i)] = psum.tile([P, 8 * P], BF16, name="ptq", tag="tq", bufs=1)
             for b in bs:
-                nc.tensor.transpose(st[("ptq", i)][:, b * P:(b + 1) * P], q_sb[c][:, t, :].bitcast(F32)[:, b * P:(b + 1) * P], ident[:])
+                nc.tensor.transpose(st[("ptq", i)][:, b * P:(b + 1) * P], q_sb[c][:, t, b * P:(b + 1) * P], ident_bf[:])
 
         def copy_q(i):
             if not ok(i):
                 return
-            st[("qT", i)] = work.tile([P, 4 * P], F32, name="qT", tag="qT", bufs=3)
+            st[("qT", i)] = work.tile([P, 8 * P], BF16, name="qT", tag="qT", bufs=3)
             nc.scalar.copy(out=st[("qT", i)][:], in_=st[("ptq", i)][:])
 
         def mm(i, h, js):
@@ -159,10 +157,9 @@ def tile_hopfieldmemorylayer_pb_t_kernel(tc, q_scaled, k, v, norm_retrieved_w, q
                 return
             if ("s", i, h) not in st:
                 st[("s", i, h)] = psum.tile([P, M], F32, name="ps_s", tag="s", bufs=2)
-            qb = st[("qT", i)][:].bitcast(BF16).rearrange("p (b r s) -> p b r s", b=4, s=2)
             for j in js:
-                g, eps = divmod(j, 2)
-                nc.tensor.matmul(out=st[("s", i, h)][:], lhsT=qb[:, 2 * h + g, :, eps], rhs=kT[h][:, g, eps, :],
+                b = 4 * h + j
+                nc.tensor.matmul(out=st[("s", i, h)][:], lhsT=st[("qT", i)][:, b * P:(b + 1) * P], rhs=kT[h][:, j, :],
                                  start=(j == 0), stop=(j == 3))
 
         def negmax(i, h):

@@ -27,40 +27,38 @@ EPS = 1e-6
 FLOPS = 2 * R * M * D * H * 2
 
 E_WORDS = True
-CE_V_EVERY = 4
+CE_V_EVERY = 2
 ADD0_G_EVERY = 0
 SCHED = [
     ("mm", 0, (0, 0), None),
     ("copy_e", 2, None, "alt"),
-    ("tq", -1, (0, 1, 2), None),
-    ("add", 5, 0, "V"),
+    ("tq", -1, (0, 1), None),
     ("mm", 0, (0, 1), None),
-    ("tq", -1, (3, 4, 5), None),
-    ("mm", 0, (0, 2), None),
-    ("tq", -1, (6, 7), None),
     ("exp", 1, 1, None),
-    ("copy_q", -1, None, None),
-    ("quant", 2, None, None),
+    ("tq", -1, (2, 3), None),
+    ("mm", 0, (0, 2), None),
     ("mm", 0, (0, 3), None),
-    ("mx", 3, 0, None),
     ("negmax", 0, 0, None),
-    ("mx", 3, 1, None),
-    ("add", 5, 1, "G"),
+    ("mx", 3, 0, None),
+    ("copy_q", -1, None, None),
+    ("add", 5, 2, "G"),
     ("store", 5, None, None),
-    ("mm", 0, (1, 0), None),
     ("sq", 3, 0, None),
+    ("mx", 3, 1, None),
+    ("recip", 2, None, None),
+    ("stt", 4, 0, None),
+    ("mm", 0, (1, 0), None),
     ("te", 1, 0, None),
-    ("mm", 0, (1, 1), None),
     ("exp", 0, 0, None),
+    ("mm", 0, (1, 1), None),
+    ("stt", 4, 1, None),
     ("te", 1, 1, None),
     ("mm", 0, (1, 2), None),
     ("sq", 3, 1, None),
-    ("chain", 3, None, None),
     ("mm", 0, (1, 3), None),
-    ("recip", 2, None, None),
-    ("stt", 4, 1, None),
-    ("stt", 4, 0, None),
     ("negmax", 0, 1, None),
+    ("quant", 2, None, None),
+    ("chain", 3, None, None),
 ]
 PIN = True
 
@@ -81,8 +79,9 @@ def tile_hopfieldmemorylayer_pb_t_kernel(tc, q_scaled, k, v, norm_retrieved_w, q
 
         ident = const.tile([P, P], F32, name="ident")
         make_identity(nc, ident[:])
-        ident_bf = const.tile([P, P], BF16, name="ident_bf")
-        make_identity(nc, ident_bf[:])
+        if not E_WORDS:
+            ident_bf = const.tile([P, P], BF16, name="ident_bf")
+            make_identity(nc, ident_bf[:])
         mhalf = const.tile([P, 1], F32, name="mhalf")
         nc.vector.memset(mhalf[:], -0.5)
         warm = const.tile([P, 1], F32, name="warm")
@@ -105,18 +104,20 @@ def tile_hopfieldmemorylayer_pb_t_kernel(tc, q_scaled, k, v, norm_retrieved_w, q
             nc.sync.dma_start(out=q_sb[c][:], in_=qv[c])
             nc.sync.dma_start(out=x_sb[c][:], in_=xv[c])
 
-        kT = [const.tile([P, 4, M], BF16, name="kT%d" % h) for h in range(H)]
+        kT = [const.tile([P, 2, 2, M], BF16, name="kT%d" % h) for h in range(H)]
         for h in range(H):
-            for gp in range(2):
-                pk = psum.tile([P, 2, M], BF16, name="pk", tag="acc", bufs=4)
-                for g2 in range(2):
-                    g = 2 * gp + g2
-                    for a in range(4):
-                        nc.tensor.transpose(pk[:, g2, a * P:(a + 1) * P], k_sb[h][:, a, g * P:(g + 1) * P], ident_bf[:])
-                for g2 in range(2):
-                    src = pk[:, g2, :].rearrange("q (p u f) -> q u p f", u=2, f=2)
-                    dst = kT[h][:, 2 * gp + g2, :].rearrange("q (u p f) -> q u p f", u=2, f=2)
-                    if g2 == 0:
+            for g in range(2):
+                pk = psum.tile([P, M], F32, name="pk", tag="acc", bufs=4)
+                for a in range(4):
+                    nc.tensor.transpose(pk[:, a * P:(a + 1) * P], k_sb[h][:, a, :].bitcast(F32)[:, g * P:(g + 1) * P], ident[:])
+                for eps in range(2):
+                    if E_WORDS:
+                        src = pk[:].bitcast(BF16).rearrange("q (p u f s) -> q s u p f", u=2, f=2, s=2)[:, eps]
+                        dst = kT[h][:, g, eps, :].rearrange("q (u p f) -> q u p f", u=2, f=2)
+                    else:
+                        src = pk[:].bitcast(BF16).rearrange("q (p t s) -> q s t p", t=4, s=2)[:, eps]
+                        dst = kT[h][:, g, eps, :].rearrange("q (t p) -> q t p", t=4)
+                    if eps == 0:
                         nc.vector.tensor_copy(out=dst, in_=src)
                     else:
                         nc.scalar.copy(out=dst, in_=src)
@@ -142,14 +143,14 @@ def tile_hopfieldmemorylayer_pb_t_kernel(tc, q_scaled, k, v, norm_retrieved_w, q
                 return
             c, t = divmod(i, TPC)
             if ("ptq", i) not in st:
-                st[("ptq", i)] = psum.tile([P, 8 * P], BF16, name="ptq", tag="tq", bufs=1)
+                st[("ptq", i)] = psum.tile([P, 4 * P], F32, name="ptq", tag="tq", bufs=1)
             for b in bs:
-                nc.tensor.transpose(st[("ptq", i)][:, b * P:(b + 1) * P], q_sb[c][:, t, b * P:(b + 1) * P], ident_bf[:])
+                nc.tensor.transpose(st[("ptq", i)][:, b * P:(b + 1) * P], q_sb[c][:, t, :].bitcast(F32)[:, b * P:(b + 1) * P], ident[:])
 
         def copy_q(i):
             if not ok(i):
                 return
-            st[("qT", i)] = work.tile([P, 8 * P], BF16, name="qT", tag="qT", bufs=3)
+            st[("qT", i)] = work.tile([P, 4 * P], F32, name="qT", tag="qT", bufs=3)
             nc.scalar.copy(out=st[("qT", i)][:], in_=st[("ptq", i)][:])
 
         def mm(i, h, js):
@@ -157,9 +158,10 @@ def tile_hopfieldmemorylayer_pb_t_kernel(tc, q_scaled, k, v, norm_retrieved_w, q
                 return
             if ("s", i, h) not in st:
                 st[("s", i, h)] = psum.tile([P, M], F32, name="ps_s", tag="s", bufs=2)
+            qb = st[("qT", i)][:].bitcast(BF16).rearrange("p (b r s) -> p b r s", b=4, s=2)
             for j in js:
-                b = 4 * h + j
-                nc.tensor.matmul(out=st[("s", i, h)][:], lhsT=st[("qT", i)][:, b * P:(b + 1) * P], rhs=kT[h][:, j, :],
+                g, eps = divmod(j, 2)
+                nc.tensor.matmul(out=st[("s", i, h)][:], lhsT=qb[:, 2 * h + g, :, eps], rhs=kT[h][:, g, eps, :],
                                  start=(j == 0), stop=(j == 3))
 
         def negmax(i, h):
@@ -265,6 +267,9 @@ def tile_hopfieldmemorylayer_pb_t_kernel(tc, q_scaled, k, v, norm_retrieved_w, q
             if not ok(i):
                 return
             c, t = divmod(i, TPC)
+            if h == 2:
+                nc.gpsimd.tensor_tensor(out=st[("o", i)][:], in0=st[("o", i)][:], in1=x_sb[c][:, t, :], op=ALU.add)
+                return
             o = st[("o", i)][:, h * D:(h + 1) * D]
             if eng == "V":
                 nc.vector.tensor_tensor(out=o, in0=o, in1=x_sb[c][:, t, h * D:(h + 1) * D], op=ALU.add)

@@ -28,37 +28,41 @@ FLOPS = 2 * R * M * D * H * 2
 
 E_WORDS = True
 CE_V_EVERY = 2
-ADD0_G_EVERY = 0
+ADD0_V_EVERY = 4
 SCHED = [
-    ("mm", 0, (0, 0), None),
     ("copy_e", 2, None, "alt"),
+    ("mm", 0, (0, 0), None),
     ("tq", -1, (0, 1), None),
     ("mm", 0, (0, 1), None),
+    ("add", 5, 0, "alt"),
+    ("add", 5, 1, "G"),
+    ("store", 5, None, None),
     ("exp", 1, 1, None),
     ("tq", -1, (2, 3), None),
     ("mm", 0, (0, 2), None),
     ("mm", 0, (0, 3), None),
-    ("negmax", 0, 0, None),
     ("mx", 3, 0, None),
-    ("copy_q", -1, None, None),
-    ("add", 5, 2, "G"),
-    ("store", 5, None, None),
-    ("sq", 3, 0, None),
-    ("mx", 3, 1, None),
     ("recip", 2, None, None),
-    ("stt", 4, 0, None),
+    ("copy_q", -1, None, None),
+    ("quant", 2, None, None),
+    ("sq", 3, 0, None),
+    ("negmax", 0, 0, None),
+    ("cc", 4, None, None),
+    ("mx", 3, 1, None),
     ("mm", 0, (1, 0), None),
-    ("te", 1, 0, None),
     ("exp", 0, 0, None),
+    ("e0", 3, None, None),
+    ("te", 1, 0, None),
     ("mm", 0, (1, 1), None),
-    ("stt", 4, 1, None),
     ("te", 1, 1, None),
-    ("mm", 0, (1, 2), None),
     ("sq", 3, 1, None),
+    ("mm", 0, (1, 2), None),
+    ("stt", 4, 1, None),
+    ("zs", 3, None, None),
+    ("stt", 4, 0, None),
+    ("pow", 3, None, None),
     ("mm", 0, (1, 3), None),
     ("negmax", 0, 1, None),
-    ("quant", 2, None, None),
-    ("chain", 3, None, None),
 ]
 PIN = True
 
@@ -84,6 +88,8 @@ def tile_hopfieldmemorylayer_pb_t_kernel(tc, q_scaled, k, v, norm_retrieved_w, q
             make_identity(nc, ident_bf[:])
         mhalf = const.tile([P, 1], F32, name="mhalf")
         nc.vector.memset(mhalf[:], -0.5)
+        epst = const.tile([P, 1], F32, name="epst")
+        nc.vector.memset(epst[:], E * EPS)
         warm = const.tile([P, 1], F32, name="warm")
         nc.scalar.activation(out=warm[:], in_=mhalf[:], func=ACT.Exp)
 
@@ -254,6 +260,23 @@ def tile_hopfieldmemorylayer_pb_t_kernel(tc, q_scaled, k, v, norm_retrieved_w, q
             nc.gpsimd.tensor_scalar(out=st[("c", i)][:], in0=st[("inv", i)][:], scalar1=rr[:, 0:1], scalar2=32.0,
                                     op0=ALU.mult, op1=ALU.mult)
 
+        def e0(i):
+            st[("e0", i)] = small.tile([P, 1], F32, name="e0t", tag="e0t")
+            nc.scalar.activation(out=st[("e0", i)][:], in_=st[("ss", i)][:, 0:1], func=ACT.Identity, bias=epst[:, 0:1], scale=1.0)
+
+        def zs(i):
+            st[("z", i)] = small.tile([P, 1], F32, name="zt", tag="zt")
+            nc.scalar.activation(out=st[("z", i)][:], in_=st[("ss", i)][:, 1:2], func=ACT.Identity, bias=st[("e0", i)][:, 0:1], scale=1.0)
+
+        def powr(i):
+            st[("rr", i)] = small.tile([P, 1], F32, name="rt", tag="rt")
+            nc.gpsimd.tensor_tensor(out=st[("rr", i)][:], in0=st[("z", i)][:], in1=mhalf[:], op=ALU.pow)
+
+        def ccv(i):
+            st[("c", i)] = small.tile([P, H], F32, name="cc", tag="cc")
+            nc.vector.tensor_scalar(out=st[("c", i)][:], in0=st[("inv", i)][:], scalar1=st[("rr", i)][:, 0:1], scalar2=32.0,
+                                    op0=ALU.mult, op1=ALU.mult)
+
         def stt(i, h):
             if not ok(i):
                 return
@@ -267,9 +290,6 @@ def tile_hopfieldmemorylayer_pb_t_kernel(tc, q_scaled, k, v, norm_retrieved_w, q
             if not ok(i):
                 return
             c, t = divmod(i, TPC)
-            if h == 2:
-                nc.gpsimd.tensor_tensor(out=st[("o", i)][:], in0=st[("o", i)][:], in1=x_sb[c][:, t, :], op=ALU.add)
-                return
             o = st[("o", i)][:, h * D:(h + 1) * D]
             if eng == "V":
                 nc.vector.tensor_tensor(out=o, in0=o, in1=x_sb[c][:, t, h * D:(h + 1) * D], op=ALU.add)
@@ -317,12 +337,20 @@ def tile_hopfieldmemorylayer_pb_t_kernel(tc, q_scaled, k, v, norm_retrieved_w, q
                     sq(i, arg)
                 elif name == "chain":
                     chain(i)
+                elif name == "e0":
+                    e0(i)
+                elif name == "zs":
+                    zs(i)
+                elif name == "pow":
+                    powr(i)
+                elif name == "cc":
+                    ccv(i)
                 elif name == "stt":
                     stt(i, arg)
                 elif name == "add":
-                    if arg == 0 and ADD0_G_EVERY > 0 and i % ADD0_G_EVERY == ADD0_G_EVERY - 1:
-                        addx(i, arg, "G")
+                    if arg == 0 and i % ADD0_V_EVERY == ADD0_V_EVERY - 1:
+                        addx(i, arg, "V")
                     else:
-                        addx(i, arg, eng)
+                        addx(i, arg, "G")
                 elif name == "store":
                     store(i)

@@ -27,43 +27,8 @@ EPS = 1e-6
 FLOPS = 2 * R * M * D * H * 2
 
 E_WORDS = True
-CE_V_EVERY = 2
-ADD0_V_EVERY = 4
-SCHED = [
-    ("copy_e", 2, None, "alt"),
-    ("mm", 0, (0, 0), None),
-    ("tq", -1, (0, 1), None),
-    ("mm", 0, (0, 1), None),
-    ("add", 5, 0, "alt"),
-    ("add", 5, 1, "G"),
-    ("store", 5, None, None),
-    ("exp", 1, 1, None),
-    ("tq", -1, (2, 3), None),
-    ("mm", 0, (0, 2), None),
-    ("mm", 0, (0, 3), None),
-    ("mx", 3, 0, None),
-    ("recip", 2, None, None),
-    ("copy_q", -1, None, None),
-    ("quant", 2, None, None),
-    ("sq", 3, 0, None),
-    ("negmax", 0, 0, None),
-    ("cc", 4, None, None),
-    ("mx", 3, 1, None),
-    ("mm", 0, (1, 0), None),
-    ("exp", 0, 0, None),
-    ("e0", 3, None, None),
-    ("te", 1, 0, None),
-    ("mm", 0, (1, 1), None),
-    ("te", 1, 1, None),
-    ("sq", 3, 1, None),
-    ("mm", 0, (1, 2), None),
-    ("stt", 4, 1, None),
-    ("zs", 3, None, None),
-    ("stt", 4, 0, None),
-    ("pow", 3, None, None),
-    ("mm", 0, (1, 3), None),
-    ("negmax", 0, 1, None),
-]
+GCOLS = 256
+VCOLS = E - GCOLS
 PIN = True
 
 
@@ -88,8 +53,8 @@ def tile_hopfieldmemorylayer_pb_t_kernel(tc, q_scaled, k, v, norm_retrieved_w, q
             make_identity(nc, ident_bf[:])
         mhalf = const.tile([P, 1], F32, name="mhalf")
         nc.vector.memset(mhalf[:], -0.5)
-        epst = const.tile([P, 1], F32, name="epst")
-        nc.vector.memset(epst[:], E * EPS)
+        mone = const.tile([P, H], F32, name="mone")
+        nc.vector.memset(mone[:], -1.0)
         warm = const.tile([P, 1], F32, name="warm")
         nc.scalar.activation(out=warm[:], in_=mhalf[:], func=ACT.Exp)
 
@@ -190,7 +155,7 @@ def tile_hopfieldmemorylayer_pb_t_kernel(tc, q_scaled, k, v, norm_retrieved_w, q
             if not ok(i):
                 return
             st[("inv", i)] = small.tile([P, H], F32, name="inv", tag="inv")
-            nc.vector.reciprocal(out=st[("inv", i)][:], in_=st[("rs", i)][:])
+            nc.gpsimd.tensor_tensor(out=st[("inv", i)][:], in0=st[("rs", i)][:], in1=mone[:], op=ALU.pow)
 
         def te(i, h, us):
             if not ok(i):
@@ -206,32 +171,29 @@ def tile_hopfieldmemorylayer_pb_t_kernel(tc, q_scaled, k, v, norm_retrieved_w, q
                 else:
                     nc.tensor.transpose(st[("pte", i)][:, h, u, :], st[("e", i)][:, h, u * P:(u + 1) * P], ident_bf[:])
 
-        def copy_e(i, eng):
+        def copy_e(i):
             if not ok(i):
                 return
             if E_WORDS:
-                st[("gq", i)] = work.tile([P, H, P, 2], F32, name="gq", tag="gq", bufs=2, align_bytes=64)
+                st[("gq", i)] = work.tile([P, H, P, 2], F32, name="gq", tag="gq", bufs=3, align_bytes=64)
             else:
-                st[("gq", i)] = work.tile([P, H, P, 4], BF16, name="gq", tag="gq", bufs=2, align_bytes=64)
-            if eng == "V":
-                nc.vector.tensor_copy(out=st[("gq", i)][:], in_=st[("pte", i)][:].rearrange("p h u r -> p h r u"))
-            else:
-                nc.scalar.copy(out=st[("gq", i)][:], in_=st[("pte", i)][:].rearrange("p h u r -> p h r u"))
+                st[("gq", i)] = work.tile([P, H, P, 4], BF16, name="gq", tag="gq", bufs=3, align_bytes=64)
+            nc.scalar.copy(out=st[("gq", i)][:], in_=st[("pte", i)][:].rearrange("p h u r -> p h r u"))
 
         def quant(i):
             if not ok(i):
                 return
-            st[("cd", i)] = work.tile([P, H * P], U32, name="cd", tag="cd", bufs=3, align_bytes=64)
-            st[("sc", i)] = work.tile([P, H * P], U8, name="sc", tag="sc", bufs=3, align_bytes=64)
+            st[("cd", i)] = work.tile([P, H * P], U32, name="cd", tag="cd", bufs=2, align_bytes=64)
+            st[("sc", i)] = work.tile([P, H * P], U8, name="sc", tag="sc", bufs=2, align_bytes=64)
             flat = st[("gq", i)][:].rearrange("p h r u -> p (h r u)")
             if E_WORDS:
                 flat = flat.bitcast(BF16)
             nc.vector.quantize_mx(out=st[("cd", i)][:].bitcast(FP8X4), scales=st[("sc", i)][:], in_=flat)
 
-        def mx(i, hs):
+        def mx(i):
             if not ok(i):
                 return
-            for h in hs:
+            for h in range(H):
                 st[("acc", i, h)] = psum.tile([P, D], F32, name="acc", tag="acc", bufs=4)
                 nc.tensor.matmul_mx(out=st[("acc", i, h)][:],
                                     lhsT=st[("cd", i)][:, h * P:(h + 1) * P].bitcast(FP8X4),
@@ -260,41 +222,27 @@ def tile_hopfieldmemorylayer_pb_t_kernel(tc, q_scaled, k, v, norm_retrieved_w, q
             nc.gpsimd.tensor_scalar(out=st[("c", i)][:], in0=st[("inv", i)][:], scalar1=rr[:, 0:1], scalar2=32.0,
                                     op0=ALU.mult, op1=ALU.mult)
 
-        def e0(i):
-            st[("e0", i)] = small.tile([P, 1], F32, name="e0t", tag="e0t")
-            nc.scalar.activation(out=st[("e0", i)][:], in_=st[("ss", i)][:, 0:1], func=ACT.Identity, bias=epst[:, 0:1], scale=1.0)
-
-        def zs(i):
-            st[("z", i)] = small.tile([P, 1], F32, name="zt", tag="zt")
-            nc.scalar.activation(out=st[("z", i)][:], in_=st[("ss", i)][:, 1:2], func=ACT.Identity, bias=st[("e0", i)][:, 0:1], scale=1.0)
-
-        def powr(i):
-            st[("rr", i)] = small.tile([P, 1], F32, name="rt", tag="rt")
-            nc.gpsimd.tensor_tensor(out=st[("rr", i)][:], in0=st[("z", i)][:], in1=mhalf[:], op=ALU.pow)
-
-        def ccv(i):
-            st[("c", i)] = small.tile([P, H], F32, name="cc", tag="cc")
-            nc.vector.tensor_scalar(out=st[("c", i)][:], in0=st[("inv", i)][:], scalar1=st[("rr", i)][:, 0:1], scalar2=32.0,
-                                    op0=ALU.mult, op1=ALU.mult)
-
-        def stt(i, h):
+        def stt(i, lo, hi):
             if not ok(i):
                 return
             if ("o", i) not in st:
                 st[("o", i)] = work.tile([P, E], F32, name="o_sb", tag="o", bufs=4)
-            nc.vector.scalar_tensor_tensor(out=st[("o", i)][:, h * D:(h + 1) * D], in0=st[("acc", i, h)][:],
-                                           scalar=st[("c", i)][:, h:h + 1], in1=w_bc[:, h * D:(h + 1) * D],
+            h = lo // D
+            nc.vector.scalar_tensor_tensor(out=st[("o", i)][:, lo:hi], in0=st[("acc", i, h)][:, lo - h * D:hi - h * D],
+                                           scalar=st[("c", i)][:, h:h + 1], in1=w_bc[:, lo:hi],
                                            op0=ALU.mult, op1=ALU.mult)
 
-        def addx(i, h, eng):
+        def add_v(i):
             if not ok(i):
                 return
             c, t = divmod(i, TPC)
-            o = st[("o", i)][:, h * D:(h + 1) * D]
-            if eng == "V":
-                nc.vector.tensor_tensor(out=o, in0=o, in1=x_sb[c][:, t, h * D:(h + 1) * D], op=ALU.add)
-            else:
-                nc.gpsimd.tensor_tensor(out=o, in0=o, in1=x_sb[c][:, t, h * D:(h + 1) * D], op=ALU.add)
+            nc.vector.tensor_tensor(out=st[("o", i)][:, 0:VCOLS], in0=st[("o", i)][:, 0:VCOLS], in1=x_sb[c][:, t, 0:VCOLS], op=ALU.add)
+
+        def add_g(i):
+            if not ok(i):
+                return
+            c, t = divmod(i, TPC)
+            nc.gpsimd.tensor_tensor(out=st[("o", i)][:, VCOLS:E], in0=st[("o", i)][:, VCOLS:E], in1=x_sb[c][:, t, VCOLS:E], op=ALU.add)
 
         def store(i):
             if not ok(i):
@@ -302,55 +250,33 @@ def tile_hopfieldmemorylayer_pb_t_kernel(tc, q_scaled, k, v, norm_retrieved_w, q
             c, t = divmod(i, TPC)
             nc.sync.dma_start(out=ov[c][:, t, :], in_=st[("o", i)][:])
 
-        for it in range(-3, NT + 9):
-            for name, lag, arg, eng in SCHED:
-                i = it - lag
-                if not ok(i):
-                    continue
-                if name == "mm":
-                    mm(i, arg[0], [arg[1]])
-                elif name == "tq":
-                    tq(i, arg)
-                elif name == "te":
-                    te(i, arg, [0, 1])
-                elif name == "mx":
-                    mx(i, [arg])
-                elif name == "copy_q":
-                    copy_q(i)
-                elif name == "copy_e":
-                    copy_e(i, "V" if i % CE_V_EVERY == CE_V_EVERY - 1 else "S")
-                elif name == "quant":
-                    quant(i)
-                elif name == "negmax":
-                    negmax(i, arg)
-                    if i == 0 and arg == 0:
-                        v_regroup(0)
-                        v_regroup(1)
-                    if i == 1 and arg == 0:
-                        v_quant(0)
-                        v_quant(1)
-                elif name == "exp":
-                    expo(i, arg)
-                elif name == "recip":
-                    recip(i)
-                elif name == "sq":
-                    sq(i, arg)
-                elif name == "chain":
-                    chain(i)
-                elif name == "e0":
-                    e0(i)
-                elif name == "zs":
-                    zs(i)
-                elif name == "pow":
-                    powr(i)
-                elif name == "cc":
-                    ccv(i)
-                elif name == "stt":
-                    stt(i, arg)
-                elif name == "add":
-                    if arg == 0 and i % ADD0_V_EVERY == ADD0_V_EVERY - 1:
-                        addx(i, arg, "V")
-                    else:
-                        addx(i, arg, "G")
-                elif name == "store":
-                    store(i)
+        for it in range(-2, NT + 7):
+            quant(it - 3)
+            add_v(it - 6)
+            store(it - 6)
+            sq(it - 4, 0)
+            sq(it - 4, 1)
+            mm(it, 0, [0, 1, 2, 3])
+            stt(it - 5, VCOLS, E)
+            stt(it - 5, 0, D)
+            stt(it - 5, D, VCOLS)
+            add_g(it - 5)
+            chain(it - 4)
+            mm(it, 1, [0, 1, 2, 3])
+            copy_e(it - 2)
+            copy_q(it + 1)
+            mx(it - 3)
+            te(it - 1, 0, [0, 1])
+            te(it - 1, 1, [0, 1])
+            tq(it + 2, [0, 1, 2, 3])
+            negmax(it, 0)
+            if it == 0:
+                v_regroup(0)
+                v_regroup(1)
+            if it == 1:
+                v_quant(0)
+                v_quant(1)
+            expo(it, 0)
+            negmax(it, 1)
+            expo(it, 1)
+            recip(it - 1)

@@ -65,18 +65,20 @@ def tile_hopfieldmemorylayer_pb_t_kernel(tc, q_scaled, k, v, norm_retrieved_w, q
         w_bc = const.tile([P, E], BF16, name="w_bc")
         nc.sync.dma_start(out=k_sb[0][:], in_=k[0].rearrange("(a p) d -> p a d", p=P))
         nc.sync.dma_start(out=q_sb[0][:, 0:1, :], in_=qv[0][:, 0:1, :])
+        nc.sync.dma_start(out=q_sb[0][:, 1:2, :], in_=qv[0][:, 1:2, :])
         nc.sync.dma_start(out=k_sb[1][:], in_=k[1].rearrange("(a p) d -> p a d", p=P))
-        nc.sync.dma_start(out=q_sb[0][:, 1:TPC, :], in_=qv[0][:, 1:TPC, :])
+        nc.sync.dma_start(out=q_sb[0][:, 2:TPC, :], in_=qv[0][:, 2:TPC, :])
         for h in range(H):
             nc.sync.dma_start(out=v_raw[h][:], in_=v[h].rearrange("(p j) w -> p j w", j=4))
+        nc.sync.dma_start(out=q_sb[1][:], in_=qv[1])
         nc.sync.dma_start(out=w_bc[:], in_=norm_retrieved_w.partition_broadcast(P))
-        nc.sync.dma_start(out=x_sb[0][:], in_=xv[0])
-        for c in range(1, NCH):
-            nc.sync.dma_start(out=q_sb[c][:], in_=qv[c])
+        for c in range(NCH):
             nc.sync.dma_start(out=x_sb[c][:], in_=xv[c])
+            if c + 2 < NCH:
+                nc.sync.dma_start(out=q_sb[c + 2][:], in_=qv[c + 2])
 
         kT = [const.tile([P, 2, 2, M], BF16, name="kT%d" % h) for h in range(H)]
-        for h in range(H):
+        def kprep(h):
             for g in range(2):
                 pk = psum.tile([P, M], F32, name="pk", tag="acc", bufs=4)
                 for a in range(4):
@@ -250,7 +252,12 @@ def tile_hopfieldmemorylayer_pb_t_kernel(tc, q_scaled, k, v, norm_retrieved_w, q
             c, t = divmod(i, TPC)
             nc.sync.dma_start(out=ov[c][:, t, :], in_=st[("o", i)][:])
 
-        for it in range(-2, NT + 7):
+        kprep(0)
+        tq(0, [0, 1, 2, 3])
+        copy_q(0)
+        kprep(1)
+        tq(1, [0, 1, 2, 3])
+        for it in range(NT):
             quant(it - 3)
             add_v(it - 6)
             store(it - 6)
@@ -270,13 +277,28 @@ def tile_hopfieldmemorylayer_pb_t_kernel(tc, q_scaled, k, v, norm_retrieved_w, q
             te(it - 1, 1, [0, 1])
             tq(it + 2, [0, 1, 2, 3])
             negmax(it, 0)
-            if it == 0:
-                v_regroup(0)
-                v_regroup(1)
-            if it == 1:
-                v_quant(0)
-                v_quant(1)
             expo(it, 0)
             negmax(it, 1)
             expo(it, 1)
             recip(it - 1)
+            if it < H:
+                v_regroup(it)
+            if it == H:
+                v_quant(0)
+                v_quant(1)
+        for it in range(NT, NT + 7):
+            sq(it - 4, 0)
+            copy_e(it - 2)
+            te(it - 1, 0, [0, 1])
+            te(it - 1, 1, [0, 1])
+            recip(it - 1)
+            sq(it - 4, 1)
+            chain(it - 4)
+            add_v(it - 6)
+            store(it - 6)
+            stt(it - 5, VCOLS, E)
+            quant(it - 3)
+            stt(it - 5, 0, D)
+            stt(it - 5, D, VCOLS)
+            add_g(it - 5)
+            mx(it - 3)

@@ -72,10 +72,13 @@ def tile_hopfieldmemorylayer_pb_t_kernel(tc, q_scaled, k, v, norm_retrieved_w, q
             nc.sync.dma_start(out=v_raw[h][:], in_=v[h].rearrange("(p j) w -> p j w", j=4))
         nc.sync.dma_start(out=q_sb[1][:], in_=qv[1])
         nc.sync.dma_start(out=w_bc[:], in_=norm_retrieved_w.partition_broadcast(P))
-        for c in range(NCH):
-            nc.sync.dma_start(out=x_sb[c][:], in_=xv[c])
+        nc.sync.dma_start(out=x_sb[0][:], in_=xv[0])
+
+        def load(c):
             if c + 2 < NCH:
                 nc.sync.dma_start(out=q_sb[c + 2][:], in_=qv[c + 2])
+            if c + 1 < NCH:
+                nc.sync.dma_start(out=x_sb[c + 1][:], in_=xv[c + 1])
 
         kT = [const.tile([P, 2, 2, M], BF16, name="kT%d" % h) for h in range(H)]
         def kprep(h):
@@ -228,7 +231,7 @@ def tile_hopfieldmemorylayer_pb_t_kernel(tc, q_scaled, k, v, norm_retrieved_w, q
             if not ok(i):
                 return
             if ("o", i) not in st:
-                st[("o", i)] = work.tile([P, E], F32, name="o_sb", tag="o", bufs=4)
+                st[("o", i)] = work.tile([P, E], F32, name="o_sb", tag="o", bufs=6)
             h = lo // D
             nc.vector.scalar_tensor_tensor(out=st[("o", i)][:, lo:hi], in0=st[("acc", i, h)][:, lo - h * D:hi - h * D],
                                            scalar=st[("c", i)][:, h:h + 1], in1=w_bc[:, lo:hi],
@@ -261,6 +264,8 @@ def tile_hopfieldmemorylayer_pb_t_kernel(tc, q_scaled, k, v, norm_retrieved_w, q
             quant(it - 3)
             add_v(it - 6)
             store(it - 6)
+            if it % TPC == 0:
+                load(it // TPC)
             sq(it - 4, 0)
             sq(it - 4, 1)
             mm(it, 0, [0, 1, 2, 3])

@@ -27,8 +27,7 @@ EPS = 1e-6
 FLOPS = 2 * R * M * D * H * 2
 
 E_WORDS = True
-GCOLS = 256
-VCOLS = E - GCOLS
+VC = 640
 PIN = True
 
 
@@ -53,8 +52,6 @@ def tile_hopfieldmemorylayer_pb_t_kernel(tc, q_scaled, k, v, norm_retrieved_w, q
             make_identity(nc, ident_bf[:])
         mhalf = const.tile([P, 1], F32, name="mhalf")
         nc.vector.memset(mhalf[:], -0.5)
-        mone = const.tile([P, H], F32, name="mone")
-        nc.vector.memset(mone[:], -1.0)
         warm = const.tile([P, 1], F32, name="warm")
         nc.scalar.activation(out=warm[:], in_=mhalf[:], func=ACT.Exp)
 
@@ -83,7 +80,7 @@ def tile_hopfieldmemorylayer_pb_t_kernel(tc, q_scaled, k, v, norm_retrieved_w, q
         kT = [const.tile([P, 2, 2, M], BF16, name="kT%d" % h) for h in range(H)]
         def kprep(h):
             for g in range(2):
-                pk = psum.tile([P, M], F32, name="pk", tag="acc", bufs=4)
+                pk = psum.tile([P, M], F32, name="pk", tag=("acc0", "acc1")[h or g], bufs=(1, 3)[h or g])
                 for a in range(4):
                     nc.tensor.transpose(pk[:, a * P:(a + 1) * P], k_sb[h][:, a, :].bitcast(F32)[:, g * P:(g + 1) * P], ident[:])
                 for eps in range(2):
@@ -160,7 +157,7 @@ def tile_hopfieldmemorylayer_pb_t_kernel(tc, q_scaled, k, v, norm_retrieved_w, q
             if not ok(i):
                 return
             st[("inv", i)] = small.tile([P, H], F32, name="inv", tag="inv")
-            nc.gpsimd.tensor_tensor(out=st[("inv", i)][:], in0=st[("rs", i)][:], in1=mone[:], op=ALU.pow)
+            nc.vector.reciprocal(out=st[("inv", i)][:], in_=st[("rs", i)][:])
 
         def te(i, h, us):
             if not ok(i):
@@ -199,7 +196,7 @@ def tile_hopfieldmemorylayer_pb_t_kernel(tc, q_scaled, k, v, norm_retrieved_w, q
             if not ok(i):
                 return
             for h in range(H):
-                st[("acc", i, h)] = psum.tile([P, D], F32, name="acc", tag="acc", bufs=4)
+                st[("acc", i, h)] = psum.tile([P, D], F32, name="acc", tag=("acc0", "acc1")[h], bufs=(1, 3)[h])
                 nc.tensor.matmul_mx(out=st[("acc", i, h)][:],
                                     lhsT=st[("cd", i)][:, h * P:(h + 1) * P].bitcast(FP8X4),
                                     lhsT_scale=st[("sc", i)][:, h * P:(h + 1) * P],
@@ -209,45 +206,62 @@ def tile_hopfieldmemorylayer_pb_t_kernel(tc, q_scaled, k, v, norm_retrieved_w, q
         def sq(i, h):
             if not ok(i):
                 return
-            if h == 0:
+            if ("ss", i) not in st:
                 st[("ss", i)] = small.tile([P, H], F32, name="ss", tag="ss")
             junk = work.tile([P, D], BF16, name="junk", tag="junk", bufs=2)
             nc.scalar.activation(out=junk[:], in_=st[("acc", i, h)][:], func=ACT.Square,
                                  scale=st[("inv", i)][:, h:h + 1], accum_out=st[("ss", i)][:, h:h + 1])
 
-        def chain(i):
+        def zsum(i):
             if not ok(i):
                 return
-            z = small.tile([P, 1], F32, name="z", tag="z")
-            rr = small.tile([P, 1], F32, name="rr", tag="rr")
-            st[("c", i)] = small.tile([P, H], F32, name="cc", tag="cc")
-            nc.gpsimd.tensor_scalar(out=z[:], in0=st[("ss", i)][:, 0:1], scalar1=st[("ss", i)][:, 1:2], scalar2=E * EPS,
+            st[("z", i)] = small.tile([P, 1], F32, name="z", tag="z")
+            nc.vector.tensor_scalar(out=st[("z", i)][:], in0=st[("ss", i)][:, 0:1], scalar1=st[("ss", i)][:, 1:2], scalar2=E * EPS,
                                     op0=ALU.add, op1=ALU.add)
-            nc.gpsimd.tensor_tensor(out=rr[:], in0=z[:], in1=mhalf[:], op=ALU.pow)
-            nc.gpsimd.tensor_scalar(out=st[("c", i)][:], in0=st[("inv", i)][:], scalar1=rr[:, 0:1], scalar2=32.0,
-                                    op0=ALU.mult, op1=ALU.mult)
 
-        def stt(i, lo, hi):
+        def powr(i):
             if not ok(i):
                 return
-            if ("o", i) not in st:
-                st[("o", i)] = work.tile([P, E], F32, name="o_sb", tag="o", bufs=6)
-            h = lo // D
-            nc.vector.scalar_tensor_tensor(out=st[("o", i)][:, lo:hi], in0=st[("acc", i, h)][:, lo - h * D:hi - h * D],
-                                           scalar=st[("c", i)][:, h:h + 1], in1=w_bc[:, lo:hi],
-                                           op0=ALU.mult, op1=ALU.mult)
+            st[("rr", i)] = small.tile([P, 1], F32, name="rr", tag="rr")
+            nc.gpsimd.tensor_tensor(out=st[("rr", i)][:], in0=st[("z", i)][:], in1=mhalf[:], op=ALU.pow)
 
-        def add_v(i):
+        def cmul(i):
+            if not ok(i):
+                return
+            st[("c", i)] = small.tile([P, 1], F32, name="cc", tag="cc")
+            nc.vector.tensor_scalar(out=st[("c", i)][:], in0=st[("inv", i)][:, 1:2], scalar1=st[("rr", i)][:, 0:1], scalar2=None, op0=ALU.mult)
+
+        def scale0(i):
+            if not ok(i):
+                return
+            st[("o", i)] = work.tile([P, E], F32, name="o_sb", tag="o", bufs=6)
+            nc.vector.scalar_tensor_tensor(out=st[("o", i)][:, 0:D], in0=st[("acc", i, 0)][:], scalar=st[("inv", i)][:, 0:1],
+                                           in1=w_bc[:, 0:D], op0=ALU.mult, op1=ALU.mult)
+
+        def scale1(i):
+            if not ok(i):
+                return
+            nc.vector.scalar_tensor_tensor(out=st[("o", i)][:, D:E], in0=st[("acc", i, 1)][:], scalar=st[("c", i)][:, 0:1],
+                                           in1=w_bc[:, D:E], op0=ALU.mult, op1=ALU.mult)
+
+        def fin0(i):
             if not ok(i):
                 return
             c, t = divmod(i, TPC)
-            nc.vector.tensor_tensor(out=st[("o", i)][:, 0:VCOLS], in0=st[("o", i)][:, 0:VCOLS], in1=x_sb[c][:, t, 0:VCOLS], op=ALU.add)
+            nc.vector.scalar_tensor_tensor(out=st[("o", i)][:, 0:D], in0=st[("o", i)][:, 0:D], scalar=st[("rr", i)][:, 0:1],
+                                           in1=x_sb[c][:, t, 0:D], op0=ALU.mult, op1=ALU.add)
+
+        def fin1(i):
+            if not ok(i):
+                return
+            c, t = divmod(i, TPC)
+            nc.vector.tensor_tensor(out=st[("o", i)][:, D:VC], in0=st[("o", i)][:, D:VC], in1=x_sb[c][:, t, D:VC], op=ALU.add)
 
         def add_g(i):
             if not ok(i):
                 return
             c, t = divmod(i, TPC)
-            nc.gpsimd.tensor_tensor(out=st[("o", i)][:, VCOLS:E], in0=st[("o", i)][:, VCOLS:E], in1=x_sb[c][:, t, VCOLS:E], op=ALU.add)
+            nc.gpsimd.tensor_tensor(out=st[("o", i)][:, VC:E], in0=st[("o", i)][:, VC:E], in1=x_sb[c][:, t, VC:E], op=ALU.add)
 
         def store(i):
             if not ok(i):
@@ -260,50 +274,39 @@ def tile_hopfieldmemorylayer_pb_t_kernel(tc, q_scaled, k, v, norm_retrieved_w, q
         copy_q(0)
         kprep(1)
         tq(1, [0, 1, 2, 3])
-        for it in range(NT):
-            quant(it - 3)
-            add_v(it - 6)
-            store(it - 6)
-            if it % TPC == 0:
-                load(it // TPC)
-            sq(it - 4, 0)
-            sq(it - 4, 1)
-            mm(it, 0, [0, 1, 2, 3])
-            stt(it - 5, VCOLS, E)
-            stt(it - 5, 0, D)
-            stt(it - 5, D, VCOLS)
+        copy_q(1)
+        for it in range(NT + 6):
+            negmax(it - 1, 1)
+            expo(it - 1, 1)
+            scale1(it - 5)
             add_g(it - 5)
-            chain(it - 4)
-            mm(it, 1, [0, 1, 2, 3])
-            copy_e(it - 2)
-            copy_q(it + 1)
-            mx(it - 3)
-            te(it - 1, 0, [0, 1])
-            te(it - 1, 1, [0, 1])
-            tq(it + 2, [0, 1, 2, 3])
+            mm(it, 0, [0, 1, 2, 3])
+            scale0(it - 3)
+            sq(it - 3, 1)
+            sq(it - 3, 0)
+            cmul(it - 4)
             negmax(it, 0)
             expo(it, 0)
-            negmax(it, 1)
-            expo(it, 1)
+            quant(it - 2)
+            fin0(it - 5)
+            fin1(it - 5)
+            store(it - 5)
+            if it % TPC == 0:
+                load(it // TPC)
+            zsum(it - 3)
+            powr(it - 3)
             recip(it - 1)
+            tq(it + 2, [0, 1, 2, 3])
+            te(it - 1, 0, [0, 1])
+            te(it - 1, 1, [0, 1])
+            copy_e(it - 1)
+            copy_q(it + 2)
+            mm(it, 1, [0, 1, 2, 3])
+            if it == 2:
+                nc.vector.tensor_scalar(out=w_bc[:], in0=w_bc[:], scalar1=32.0, scalar2=None, op0=ALU.mult)
             if it < H:
                 v_regroup(it)
             if it == H:
                 v_quant(0)
                 v_quant(1)
-        for it in range(NT, NT + 7):
-            sq(it - 4, 0)
-            copy_e(it - 2)
-            te(it - 1, 0, [0, 1])
-            te(it - 1, 1, [0, 1])
-            recip(it - 1)
-            sq(it - 4, 1)
-            chain(it - 4)
-            add_v(it - 6)
-            store(it - 6)
-            stt(it - 5, VCOLS, E)
-            quant(it - 3)
-            stt(it - 5, 0, D)
-            stt(it - 5, D, VCOLS)
-            add_g(it - 5)
-            mx(it - 3)
+            mx(it - 2)

@@ -27,7 +27,6 @@ EPS = 1e-6
 FLOPS = 2 * R * M * D * H * 2
 
 E_WORDS = True
-VC = 640
 PIN = True
 
 
@@ -60,10 +59,10 @@ def tile_hopfieldmemorylayer_pb_t_kernel(tc, q_scaled, k, v, norm_retrieved_w, q
         q_sb = [const.tile([P, TPC, E], BF16, name="q_sb%d" % c) for c in range(NCH)]
         x_sb = [const.tile([P, TPC, E], BF16, name="x_sb%d" % c) for c in range(NCH)]
         w_bc = const.tile([P, E], BF16, name="w_bc")
-        nc.sync.dma_start(out=k_sb[0][:], in_=k[0].rearrange("(a p) d -> p a d", p=P))
         nc.sync.dma_start(out=q_sb[0][:, 0:1, :], in_=qv[0][:, 0:1, :])
-        nc.sync.dma_start(out=q_sb[0][:, 1:2, :], in_=qv[0][:, 1:2, :])
+        nc.sync.dma_start(out=k_sb[0][:], in_=k[0].rearrange("(a p) d -> p a d", p=P))
         nc.sync.dma_start(out=k_sb[1][:], in_=k[1].rearrange("(a p) d -> p a d", p=P))
+        nc.sync.dma_start(out=q_sb[0][:, 1:2, :], in_=qv[0][:, 1:2, :])
         nc.sync.dma_start(out=q_sb[0][:, 2:TPC, :], in_=qv[0][:, 2:TPC, :])
         for h in range(H):
             nc.sync.dma_start(out=v_raw[h][:], in_=v[h].rearrange("(p j) w -> p j w", j=4))
@@ -100,7 +99,8 @@ def tile_hopfieldmemorylayer_pb_t_kernel(tc, q_scaled, k, v, norm_retrieved_w, q
         v_grp = [const.tile([P, D, 4], BF16, name="v_grp%d" % h, align_bytes=64) for h in range(H)]
 
         def v_regroup(h):
-            nc.vector.tensor_copy(out=v_grp[h][:], in_=v_raw[h][:].rearrange("p j w -> p w j"))
+            nc.gpsimd.tensor_scalar(out=v_grp[h][:], in0=v_raw[h][:].rearrange("p j w -> p w j"), scalar1=1.0, scalar2=0.0,
+                                    op0=ALU.mult, op1=ALU.add)
 
         def v_quant(h):
             nc.vector.quantize_mx(out=v_codes[h][:].bitcast(FP8X4), scales=v_scales[h][:],
@@ -196,7 +196,10 @@ def tile_hopfieldmemorylayer_pb_t_kernel(tc, q_scaled, k, v, norm_retrieved_w, q
             if not ok(i):
                 return
             for h in range(H):
-                st[("acc", i, h)] = psum.tile([P, D], F32, name="acc", tag=("acc0", "acc1")[h], bufs=(1, 3)[h])
+                if i == NT - 2:
+                    st[("acc", i, h)] = psum.tile([P, D], F32, name="acc", tag="s", bufs=2)
+                else:
+                    st[("acc", i, h)] = psum.tile([P, D], F32, name="acc", tag=("acc0", "acc1")[h], bufs=(1, 3)[h])
                 nc.tensor.matmul_mx(out=st[("acc", i, h)][:],
                                     lhsT=st[("cd", i)][:, h * P:(h + 1) * P].bitcast(FP8X4),
                                     lhsT_scale=st[("sc", i)][:, h * P:(h + 1) * P],
@@ -244,6 +247,21 @@ def tile_hopfieldmemorylayer_pb_t_kernel(tc, q_scaled, k, v, norm_retrieved_w, q
             nc.vector.scalar_tensor_tensor(out=st[("o", i)][:, D:E], in0=st[("acc", i, 1)][:], scalar=st[("c", i)][:, 0:1],
                                            in1=w_bc[:, D:E], op0=ALU.mult, op1=ALU.mult)
 
+        def scale1i(i):
+            if not ok(i):
+                return
+            nc.vector.scalar_tensor_tensor(out=st[("o", i)][:, D:E], in0=st[("acc", i, 1)][:], scalar=st[("inv", i)][:, 1:2],
+                                           in1=w_bc[:, D:E], op0=ALU.mult, op1=ALU.mult)
+
+        def fin(i, lo, hi):
+            c, t = divmod(i, TPC)
+            nc.vector.scalar_tensor_tensor(out=st[("o", i)][:, lo:hi], in0=st[("o", i)][:, lo:hi], scalar=st[("rr", i)][:, 0:1],
+                                           in1=x_sb[c][:, t, lo:hi], op0=ALU.mult, op1=ALU.add)
+
+        def store_part(i, lo, hi):
+            c, t = divmod(i, TPC)
+            nc.sync.dma_start(out=ov[c][:, t, lo:hi], in_=st[("o", i)][:, lo:hi])
+
         def fin0(i):
             if not ok(i):
                 return
@@ -251,17 +269,15 @@ def tile_hopfieldmemorylayer_pb_t_kernel(tc, q_scaled, k, v, norm_retrieved_w, q
             nc.vector.scalar_tensor_tensor(out=st[("o", i)][:, 0:D], in0=st[("o", i)][:, 0:D], scalar=st[("rr", i)][:, 0:1],
                                            in1=x_sb[c][:, t, 0:D], op0=ALU.mult, op1=ALU.add)
 
-        def fin1(i):
-            if not ok(i):
-                return
+        def add_v(i):
             c, t = divmod(i, TPC)
-            nc.vector.tensor_tensor(out=st[("o", i)][:, D:VC], in0=st[("o", i)][:, D:VC], in1=x_sb[c][:, t, D:VC], op=ALU.add)
+            nc.vector.tensor_tensor(out=st[("o", i)][:, D:E], in0=st[("o", i)][:, D:E], in1=x_sb[c][:, t, D:E], op=ALU.add)
 
         def add_g(i):
             if not ok(i):
                 return
             c, t = divmod(i, TPC)
-            nc.gpsimd.tensor_tensor(out=st[("o", i)][:, VC:E], in0=st[("o", i)][:, VC:E], in1=x_sb[c][:, t, VC:E], op=ALU.add)
+            nc.gpsimd.tensor_tensor(out=st[("o", i)][:, D:E], in0=st[("o", i)][:, D:E], in1=x_sb[c][:, t, D:E], op=ALU.add)
 
         def store(i):
             if not ok(i):
@@ -269,44 +285,76 @@ def tile_hopfieldmemorylayer_pb_t_kernel(tc, q_scaled, k, v, norm_retrieved_w, q
             c, t = divmod(i, TPC)
             nc.sync.dma_start(out=ov[c][:, t, :], in_=st[("o", i)][:])
 
-        kprep(0)
+        v_regroup(0)
+        v_regroup(1)
         tq(0, [0, 1, 2, 3])
         copy_q(0)
+        kprep(0)
         kprep(1)
         tq(1, [0, 1, 2, 3])
         copy_q(1)
-        for it in range(NT + 6):
-            negmax(it - 1, 1)
-            expo(it - 1, 1)
-            scale1(it - 5)
-            add_g(it - 5)
-            mm(it, 0, [0, 1, 2, 3])
+        for it in range(NT):
             scale0(it - 3)
+            cmul(it - 4)
+            mm(it, 0, [0, 1, 2, 3])
             sq(it - 3, 1)
             sq(it - 3, 0)
-            cmul(it - 4)
             negmax(it, 0)
             expo(it, 0)
             quant(it - 2)
-            fin0(it - 5)
-            fin1(it - 5)
+            if it == 2:
+                v_quant(0)
+                v_quant(1)
+            fin0(it - 4)
             store(it - 5)
             if it % TPC == 0:
                 load(it // TPC)
             zsum(it - 3)
             powr(it - 3)
             recip(it - 1)
+            scale1(it - 4)
+            add_g(it - 4)
             tq(it + 2, [0, 1, 2, 3])
             te(it - 1, 0, [0, 1])
             te(it - 1, 1, [0, 1])
             copy_e(it - 1)
             copy_q(it + 2)
             mm(it, 1, [0, 1, 2, 3])
-            if it == 2:
+            negmax(it, 1)
+            expo(it, 1)
+            if it == 1:
                 nc.vector.tensor_scalar(out=w_bc[:], in0=w_bc[:], scalar1=32.0, scalar2=None, op0=ALU.mult)
-            if it < H:
-                v_regroup(it)
-            if it == H:
-                v_quant(0)
-                v_quant(1)
             mx(it - 2)
+        n = NT
+        te(n - 1, 0, [0, 1])
+        te(n - 1, 1, [0, 1])
+        scale0(n - 3)
+        cmul(n - 4)
+        scale1i(n - 3)
+        sq(n - 3, 0)
+        copy_e(n - 1)
+        sq(n - 3, 1)
+        quant(n - 2)
+        mx(n - 2)
+        store(n - 5)
+        scale1(n - 4)
+        recip(n - 1)
+        quant(n - 1)
+        mx(n - 1)
+        fin0(n - 4)
+        zsum(n - 3)
+        powr(n - 3)
+        add_v(n - 4)
+        store(n - 4)
+        for i in (n - 2, n - 1):
+            sq(i, 0)
+            sq(i, 1)
+            scale0(i)
+            zsum(i)
+            powr(i)
+            scale1i(i)
+        for i in range(n - 3, n):
+            fin(i, 0, D)
+            store_part(i, 0, D)
+            fin(i, D, E)
+            store_part(i, D, E)

@@ -52,6 +52,8 @@ def tile_hopfieldmemorylayer_pb_t_kernel(tc, q_scaled, k, v, norm_retrieved_w, q
         mhalf = const.tile([P, 1], F32, name="mhalf")
         nc.vector.memset(mhalf[:], -0.5)
         warm = const.tile([P, 1], F32, name="warm")
+        wz = const.tile([P, M], BF16, name="wz")
+        nc.vector.memset(wz[:], 0.0)
         nc.scalar.activation(out=warm[:], in_=mhalf[:], func=ACT.Exp)
 
         k_sb = [const.tile([P, 4, D], BF16, name="k_sb%d" % h) for h in range(H)]
@@ -285,11 +287,19 @@ def tile_hopfieldmemorylayer_pb_t_kernel(tc, q_scaled, k, v, norm_retrieved_w, q
             c, t = divmod(i, TPC)
             nc.sync.dma_start(out=ov[c][:, t, :], in_=st[("o", i)][:])
 
+        def warm_up(n):
+            for rep in range(n):
+                ps_w = psum.tile([P, M], F32, name="ps_w", tag="s", bufs=2)
+                nc.tensor.matmul(out=ps_w[:], lhsT=wz[:, 0:P], rhs=wz[:], start=True, stop=True)
+
         v_regroup(0)
         v_regroup(1)
+        warm_up(4)
         tq(0, [0, 1, 2, 3])
         copy_q(0)
+        warm_up(1)
         kprep(0)
+        warm_up(1)
         kprep(1)
         tq(1, [0, 1, 2, 3])
         copy_q(1)

@@ -62,8 +62,9 @@ def tile_hopfieldmemorylayer_pb_t_kernel(tc, q_scaled, k, v, norm_retrieved_w, q
         x_sb = [const.tile([P, TPC, E], BF16, name="x_sb%d" % c) for c in range(NCH)]
         w_bc = const.tile([P, E], BF16, name="w_bc")
         nc.sync.dma_start(out=q_sb[0][:, 0:1, :], in_=qv[0][:, 0:1, :])
-        nc.sync.dma_start(out=k_sb[0][:], in_=k[0].rearrange("(a p) d -> p a d", p=P))
-        nc.sync.dma_start(out=k_sb[1][:], in_=k[1].rearrange("(a p) d -> p a d", p=P))
+        for h in range(H):
+            for a in (0, 2):
+                nc.sync.dma_start(out=k_sb[h][:, a:a + 2, :], in_=k[h].rearrange("(a p) d -> p a d", p=P)[:, a:a + 2, :])
         nc.sync.dma_start(out=q_sb[0][:, 1:2, :], in_=qv[0][:, 1:2, :])
         nc.sync.dma_start(out=q_sb[0][:, 2:TPC, :], in_=qv[0][:, 2:TPC, :])
         for h in range(H):
@@ -80,10 +81,15 @@ def tile_hopfieldmemorylayer_pb_t_kernel(tc, q_scaled, k, v, norm_retrieved_w, q
 
         kT = [const.tile([P, 2, 2, M], BF16, name="kT%d" % h) for h in range(H)]
         def kprep(h):
+            pks = []
             for g in range(2):
                 pk = psum.tile([P, M], F32, name="pk", tag=("acc0", "acc1")[h or g], bufs=(1, 3)[h or g])
-                for a in range(4):
-                    nc.tensor.transpose(pk[:, a * P:(a + 1) * P], k_sb[h][:, a, :].bitcast(F32)[:, g * P:(g + 1) * P], ident[:])
+                pks.append(pk)
+            for a in range(4):
+                for g in range(2):
+                    nc.tensor.transpose(pks[g][:, a * P:(a + 1) * P], k_sb[h][:, a, :].bitcast(F32)[:, g * P:(g + 1) * P], ident[:])
+            for g in range(2):
+                pk = pks[g]
                 for eps in range(2):
                     if E_WORDS:
                         src = pk[:].bitcast(BF16).rearrange("q (p u f s) -> q s u p f", u=2, f=2, s=2)[:, eps]
@@ -96,9 +102,9 @@ def tile_hopfieldmemorylayer_pb_t_kernel(tc, q_scaled, k, v, norm_retrieved_w, q
                     else:
                         nc.scalar.copy(out=dst, in_=src)
 
-        v_codes = [const.tile([P, D], U32, name="v_codes%d" % h, align_bytes=64) for h in range(H)]
-        v_scales = [const.tile([P, D], U8, name="v_scales%d" % h, align_bytes=64) for h in range(H)]
-        v_grp = [const.tile([P, D, 4], BF16, name="v_grp%d" % h, align_bytes=64) for h in range(H)]
+        v_codes = [const.tile([P, D], U32, name="v_codes%d" % h, align_bytes=256) for h in range(H)]
+        v_scales = [const.tile([P, D], U8, name="v_scales%d" % h, align_bytes=256) for h in range(H)]
+        v_grp = [const.tile([P, D, 4], BF16, name="v_grp%d" % h, align_bytes=256) for h in range(H)]
 
         def v_regroup(h):
             nc.gpsimd.tensor_scalar(out=v_grp[h][:], in0=v_raw[h][:].rearrange("p j w -> p w j"), scalar1=1.0, scalar2=0.0,
@@ -179,16 +185,16 @@ def tile_hopfieldmemorylayer_pb_t_kernel(tc, q_scaled, k, v, norm_retrieved_w, q
             if not ok(i):
                 return
             if E_WORDS:
-                st[("gq", i)] = work.tile([P, H, P, 2], F32, name="gq", tag="gq", bufs=3, align_bytes=64)
+                st[("gq", i)] = work.tile([P, H, P, 2], F32, name="gq", tag="gq", bufs=3, align_bytes=256)
             else:
-                st[("gq", i)] = work.tile([P, H, P, 4], BF16, name="gq", tag="gq", bufs=3, align_bytes=64)
+                st[("gq", i)] = work.tile([P, H, P, 4], BF16, name="gq", tag="gq", bufs=3, align_bytes=256)
             nc.scalar.copy(out=st[("gq", i)][:], in_=st[("pte", i)][:].rearrange("p h u r -> p h r u"))
 
         def quant(i):
             if not ok(i):
                 return
-            st[("cd", i)] = work.tile([P, H * P], U32, name="cd", tag="cd", bufs=2, align_bytes=64)
-            st[("sc", i)] = work.tile([P, H * P], U8, name="sc", tag="sc", bufs=2, align_bytes=64)
+            st[("cd", i)] = work.tile([P, H * P], U32, name="cd", tag="cd", bufs=2, align_bytes=256)
+            st[("sc", i)] = work.tile([P, H * P], U8, name="sc", tag="sc", bufs=2, align_bytes=256)
             flat = st[("gq", i)][:].rearrange("p h r u -> p (h r u)")
             if E_WORDS:
                 flat = flat.bitcast(BF16)
@@ -301,12 +307,13 @@ def tile_hopfieldmemorylayer_pb_t_kernel(tc, q_scaled, k, v, norm_retrieved_w, q
         kprep(0)
         warm_up(1)
         kprep(1)
-        tq(1, [0, 1, 2, 3])
-        copy_q(1)
         for it in range(NT):
             scale0(it - 3)
             cmul(it - 4)
             mm(it, 0, [0, 1, 2, 3])
+            if it == 0:
+                tq(1, [0, 1, 2, 3])
+                copy_q(1)
             sq(it - 3, 1)
             sq(it - 3, 0)
             negmax(it, 0)
@@ -324,12 +331,15 @@ def tile_hopfieldmemorylayer_pb_t_kernel(tc, q_scaled, k, v, norm_retrieved_w, q
             recip(it - 1)
             scale1(it - 4)
             add_g(it - 4)
+            if it == 0:
+                mm(it, 1, [0, 1, 2, 3])
             tq(it + 2, [0, 1, 2, 3])
             te(it - 1, 0, [0, 1])
             te(it - 1, 1, [0, 1])
             copy_e(it - 1)
             copy_q(it + 2)
-            mm(it, 1, [0, 1, 2, 3])
+            if it > 0:
+                mm(it, 1, [0, 1, 2, 3])
             negmax(it, 1)
             expo(it, 1)
             if it == 1:

@@ -83,7 +83,7 @@ def tile_hopfieldmemorylayer_pb_t_kernel(tc, q_scaled, k, v, norm_retrieved_w, q
         def kprep(h):
             pks = []
             for g in range(2):
-                pk = psum.tile([P, M], F32, name="pk", tag=("acc0", "acc1")[h or g], bufs=(1, 3)[h or g])
+                pk = psum.tile([P, M], F32, name="pk", tag=("acc0", "acc1", "acc1", "s")[2 * h + g], bufs=(1, 2, 2, 3)[2 * h + g])
                 pks.append(pk)
             for a in range(4):
                 for g in range(2):
@@ -138,12 +138,26 @@ def tile_hopfieldmemorylayer_pb_t_kernel(tc, q_scaled, k, v, norm_retrieved_w, q
             if not ok(i):
                 return
             if ("s", i, h) not in st:
-                st[("s", i, h)] = psum.tile([P, M], F32, name="ps_s", tag="s", bufs=2)
+                st[("s", i, h)] = psum.tile([P, M], F32, name="ps_s", tag="s", bufs=3)
             qb = st[("qT", i)][:].bitcast(BF16).rearrange("p (b r s) -> p b r s", b=4, s=2)
             for j in js:
                 g, eps = divmod(j, 2)
                 nc.tensor.matmul(out=st[("s", i, h)][:], lhsT=qb[:, 2 * h + g, :, eps], rhs=kT[h][:, g, eps, :],
                                  start=(j == 0), stop=(j == 3))
+
+        def mm_q(i):
+            for j in range(4):
+                mm(i, 0, [j])
+                tq(i + 2, [j])
+
+        def mm_e(i):
+            mm(i, 1, [0])
+            te(i - 1, 0, [0])
+            mm(i, 1, [1])
+            te(i - 1, 0, [1])
+            mm(i, 1, [2])
+            te(i - 1, 1, [0, 1])
+            mm(i, 1, [3])
 
         def negmax(i, h):
             if not ok(i):
@@ -205,9 +219,9 @@ def tile_hopfieldmemorylayer_pb_t_kernel(tc, q_scaled, k, v, norm_retrieved_w, q
                 return
             for h in range(H):
                 if i == NT - 2:
-                    st[("acc", i, h)] = psum.tile([P, D], F32, name="acc", tag="s", bufs=2)
+                    st[("acc", i, h)] = psum.tile([P, D], F32, name="acc", tag="s", bufs=3)
                 else:
-                    st[("acc", i, h)] = psum.tile([P, D], F32, name="acc", tag=("acc0", "acc1")[h], bufs=(1, 3)[h])
+                    st[("acc", i, h)] = psum.tile([P, D], F32, name="acc", tag=("acc0", "acc1")[h], bufs=(1, 2)[h])
                 nc.tensor.matmul_mx(out=st[("acc", i, h)][:],
                                     lhsT=st[("cd", i)][:, h * P:(h + 1) * P].bitcast(FP8X4),
                                     lhsT_scale=st[("sc", i)][:, h * P:(h + 1) * P],
@@ -295,7 +309,7 @@ def tile_hopfieldmemorylayer_pb_t_kernel(tc, q_scaled, k, v, norm_retrieved_w, q
 
         def warm_up(n):
             for rep in range(n):
-                ps_w = psum.tile([P, M], F32, name="ps_w", tag="s", bufs=2)
+                ps_w = psum.tile([P, M], F32, name="ps_w", tag="s", bufs=3)
                 nc.tensor.matmul(out=ps_w[:], lhsT=wz[:, 0:P], rhs=wz[:], start=True, stop=True)
 
         v_regroup(0)
@@ -310,10 +324,14 @@ def tile_hopfieldmemorylayer_pb_t_kernel(tc, q_scaled, k, v, norm_retrieved_w, q
         for it in range(NT):
             scale0(it - 3)
             cmul(it - 4)
-            mm(it, 0, [0, 1, 2, 3])
+            recip(it - 2)
+            scale1(it - 4)
             if it == 0:
+                mm(it, 0, [0, 1, 2, 3])
                 tq(1, [0, 1, 2, 3])
                 copy_q(1)
+            else:
+                mm_q(it)
             sq(it - 3, 1)
             sq(it - 3, 0)
             negmax(it, 0)
@@ -323,23 +341,17 @@ def tile_hopfieldmemorylayer_pb_t_kernel(tc, q_scaled, k, v, norm_retrieved_w, q
                 v_quant(0)
                 v_quant(1)
             fin0(it - 4)
+            zsum(it - 3)
+            powr(it - 3)
+            add_g(it - 4)
             store(it - 5)
             if it % TPC == 0:
                 load(it // TPC)
-            zsum(it - 3)
-            powr(it - 3)
-            recip(it - 1)
-            scale1(it - 4)
-            add_g(it - 4)
+            mm_e(it)
             if it == 0:
-                mm(it, 1, [0, 1, 2, 3])
-            tq(it + 2, [0, 1, 2, 3])
-            te(it - 1, 0, [0, 1])
-            te(it - 1, 1, [0, 1])
-            copy_e(it - 1)
+                tq(2, [0, 1, 2, 3])
             copy_q(it + 2)
-            if it > 0:
-                mm(it, 1, [0, 1, 2, 3])
+            copy_e(it - 1)
             negmax(it, 1)
             expo(it, 1)
             if it == 1:
@@ -348,8 +360,10 @@ def tile_hopfieldmemorylayer_pb_t_kernel(tc, q_scaled, k, v, norm_retrieved_w, q
         n = NT
         te(n - 1, 0, [0, 1])
         te(n - 1, 1, [0, 1])
-        scale0(n - 3)
         cmul(n - 4)
+        recip(n - 2)
+        scale0(n - 3)
+        scale1(n - 4)
         scale1i(n - 3)
         sq(n - 3, 0)
         copy_e(n - 1)
@@ -357,7 +371,6 @@ def tile_hopfieldmemorylayer_pb_t_kernel(tc, q_scaled, k, v, norm_retrieved_w, q
         quant(n - 2)
         mx(n - 2)
         store(n - 5)
-        scale1(n - 4)
         recip(n - 1)
         quant(n - 1)
         mx(n - 1)

@@ -330,6 +330,9 @@ def tile_hopfieldmemorylayer_pb_t_kernel(tc, q_scaled, k, v, norm_retrieved_w, q
                 mm(it, 0, [0, 1, 2, 3])
                 tq(1, [0, 1, 2, 3])
                 copy_q(1)
+            elif it < 3:
+                mm(it, 0, [0, 1, 2, 3])
+                tq(it + 2, [0, 1, 2, 3])
             else:
                 mm_q(it)
             sq(it - 3, 1)
@@ -337,9 +340,6 @@ def tile_hopfieldmemorylayer_pb_t_kernel(tc, q_scaled, k, v, norm_retrieved_w, q
             negmax(it, 0)
             expo(it, 0)
             quant(it - 2)
-            if it == 2:
-                v_quant(0)
-                v_quant(1)
             fin0(it - 4)
             zsum(it - 3)
             powr(it - 3)
@@ -355,16 +355,19 @@ def tile_hopfieldmemorylayer_pb_t_kernel(tc, q_scaled, k, v, norm_retrieved_w, q
             negmax(it, 1)
             expo(it, 1)
             if it == 1:
+                v_quant(0)
+                v_quant(1)
+            if it == 2:
                 nc.vector.tensor_scalar(out=w_bc[:], in0=w_bc[:], scalar1=32.0, scalar2=None, op0=ALU.mult)
             mx(it - 2)
         n = NT
         te(n - 1, 0, [0, 1])
         te(n - 1, 1, [0, 1])
-        cmul(n - 4)
-        recip(n - 2)
         scale0(n - 3)
-        scale1(n - 4)
+        cmul(n - 4)
         scale1i(n - 3)
+        recip(n - 2)
+        scale1(n - 4)
         sq(n - 3, 0)
         copy_e(n - 1)
         sq(n - 3, 1)
@@ -379,15 +382,28 @@ def tile_hopfieldmemorylayer_pb_t_kernel(tc, q_scaled, k, v, norm_retrieved_w, q
         powr(n - 3)
         add_v(n - 4)
         store(n - 4)
-        for i in (n - 2, n - 1):
-            sq(i, 0)
-            sq(i, 1)
-            scale0(i)
-            zsum(i)
-            powr(i)
-            scale1i(i)
-        for i in range(n - 3, n):
-            fin(i, 0, D)
-            store_part(i, 0, D)
-            fin(i, D, E)
-            store_part(i, D, E)
+        sq(n - 2, 0)
+        sq(n - 2, 1)
+        scale0(n - 2)
+        scale1i(n - 2)
+        zsum(n - 2)
+        fin(n - 3, 0, D)
+        store_part(n - 3, 0, D)
+        powr(n - 2)
+        sq(n - 1, 0)
+        sq(n - 1, 1)
+        scale0(n - 1)
+        fin(n - 3, D, E)
+        store_part(n - 3, D, E)
+        zsum(n - 1)
+        powr(n - 1)
+        fin(n - 2, 0, D)
+        store_part(n - 2, 0, D)
+        scale1i(n - 1)
+        fin(n - 2, D, E)
+        store_part(n - 2, D, E)
+        fin(n - 1, 0, D)
+        store_part(n - 1, 0, D)
+        for lo in (D, D + D // 2):
+            fin(n - 1, lo, lo + D // 2)
+            store_part(n - 1, lo, lo + D // 2)

@@ -46,9 +46,8 @@ def tile_hopfieldmemorylayer_pb_t_kernel(tc, q_scaled, k, v, norm_retrieved_w, q
 
         ident = const.tile([P, P], F32, name="ident")
         make_identity(nc, ident[:])
-        if not E_WORDS:
-            ident_bf = const.tile([P, P], BF16, name="ident_bf")
-            make_identity(nc, ident_bf[:])
+        ident_bf = const.tile([P, P], BF16, name="ident_bf")
+        make_identity(nc, ident_bf[:])
         mhalf = const.tile([P, 1], F32, name="mhalf")
         nc.vector.memset(mhalf[:], -0.5)
         warm = const.tile([P, 1], F32, name="warm")
@@ -83,20 +82,16 @@ def tile_hopfieldmemorylayer_pb_t_kernel(tc, q_scaled, k, v, norm_retrieved_w, q
         def kprep(h):
             pks = []
             for g in range(2):
-                pk = psum.tile([P, M], F32, name="pk", tag=("acc0", "acc1", "acc1", "s")[2 * h + g], bufs=(1, 2, 2, 3)[2 * h + g])
+                pk = psum.tile([P, 2, M], BF16, name="pk", tag=("acc0", "acc1", "acc1", "s")[2 * h + g], bufs=(1, 2, 2, 3)[2 * h + g])
                 pks.append(pk)
             for a in range(4):
-                for g in range(2):
-                    nc.tensor.transpose(pks[g][:, a * P:(a + 1) * P], k_sb[h][:, a, :].bitcast(F32)[:, g * P:(g + 1) * P], ident[:])
+                for j in range(4):
+                    nc.tensor.transpose(pks[j // 2][:, j % 2, a * P:(a + 1) * P], k_sb[h][:, a, j * P:(j + 1) * P], ident_bf[:])
             for g in range(2):
                 pk = pks[g]
                 for eps in range(2):
-                    if E_WORDS:
-                        src = pk[:].bitcast(BF16).rearrange("q (p u f s) -> q s u p f", u=2, f=2, s=2)[:, eps]
-                        dst = kT[h][:, g, eps, :].rearrange("q (u p f) -> q u p f", u=2, f=2)
-                    else:
-                        src = pk[:].bitcast(BF16).rearrange("q (p t s) -> q s t p", t=4, s=2)[:, eps]
-                        dst = kT[h][:, g, eps, :].rearrange("q (t p) -> q t p", t=4)
+                    src = pk[:, eps, :].rearrange("q (p u f) -> q u p f", u=2, f=2)
+                    dst = kT[h][:, g, eps, :].rearrange("q (u p f) -> q u p f", u=2, f=2)
                     if eps == 0:
                         nc.vector.tensor_copy(out=dst, in_=src)
                     else:
@@ -124,14 +119,15 @@ def tile_hopfieldmemorylayer_pb_t_kernel(tc, q_scaled, k, v, norm_retrieved_w, q
                 return
             c, t = divmod(i, TPC)
             if ("ptq", i) not in st:
-                st[("ptq", i)] = psum.tile([P, 4 * P], F32, name="ptq", tag="tq", bufs=1)
+                st[("ptq", i)] = psum.tile([P, 8 * P], BF16, name="ptq", tag="tq", bufs=1)
             for b in bs:
-                nc.tensor.transpose(st[("ptq", i)][:, b * P:(b + 1) * P], q_sb[c][:, t, :].bitcast(F32)[:, b * P:(b + 1) * P], ident[:])
+                for b2 in (2 * b, 2 * b + 1):
+                    nc.tensor.transpose(st[("ptq", i)][:, b2 * P:(b2 + 1) * P], q_sb[c][:, t, b2 * P:(b2 + 1) * P], ident_bf[:])
 
         def copy_q(i):
             if not ok(i):
                 return
-            st[("qT", i)] = work.tile([P, 4 * P], F32, name="qT", tag="qT", bufs=3)
+            st[("qT", i)] = work.tile([P, 8 * P], BF16, name="qT", tag="qT", bufs=3)
             nc.scalar.copy(out=st[("qT", i)][:], in_=st[("ptq", i)][:])
 
         def mm(i, h, js):
@@ -139,10 +135,10 @@ def tile_hopfieldmemorylayer_pb_t_kernel(tc, q_scaled, k, v, norm_retrieved_w, q
                 return
             if ("s", i, h) not in st:
                 st[("s", i, h)] = psum.tile([P, M], F32, name="ps_s", tag="s", bufs=3)
-            qb = st[("qT", i)][:].bitcast(BF16).rearrange("p (b r s) -> p b r s", b=4, s=2)
+            qb = st[("qT", i)][:].rearrange("p (b r) -> p b r", b=8)
             for j in js:
                 g, eps = divmod(j, 2)
-                nc.tensor.matmul(out=st[("s", i, h)][:], lhsT=qb[:, 2 * h + g, :, eps], rhs=kT[h][:, g, eps, :],
+                nc.tensor.matmul(out=st[("s", i, h)][:], lhsT=qb[:, 4 * h + j, :], rhs=kT[h][:, g, eps, :],
                                  start=(j == 0), stop=(j == 3))
 
         def mm_q(i):

@@ -64,10 +64,11 @@ def tile_hopfieldmemorylayer_pb_t_kernel(tc, q_scaled, k, v, norm_retrieved_w, q
         for h in range(H):
             for a in (0, 2):
                 nc.sync.dma_start(out=k_sb[h][:, a:a + 2, :], in_=k[h].rearrange("(a p) d -> p a d", p=P)[:, a:a + 2, :])
+        nc.sync.dma_start(out=v_raw[0][:], in_=v[0].rearrange("(p j) w -> p j w", j=4))
         nc.sync.dma_start(out=q_sb[0][:, 1:2, :], in_=qv[0][:, 1:2, :])
-        nc.sync.dma_start(out=q_sb[0][:, 2:TPC, :], in_=qv[0][:, 2:TPC, :])
-        for h in range(H):
-            nc.sync.dma_start(out=v_raw[h][:], in_=v[h].rearrange("(p j) w -> p j w", j=4))
+        nc.sync.dma_start(out=q_sb[0][:, 2:3, :], in_=qv[0][:, 2:3, :])
+        nc.sync.dma_start(out=v_raw[1][:], in_=v[1].rearrange("(p j) w -> p j w", j=4))
+        nc.sync.dma_start(out=q_sb[0][:, 3:TPC, :], in_=qv[0][:, 3:TPC, :])
         nc.sync.dma_start(out=q_sb[1][:], in_=qv[1])
         nc.sync.dma_start(out=w_bc[:], in_=norm_retrieved_w.partition_broadcast(P))
         nc.sync.dma_start(out=x_sb[0][:], in_=xv[0])
@@ -92,7 +93,7 @@ def tile_hopfieldmemorylayer_pb_t_kernel(tc, q_scaled, k, v, norm_retrieved_w, q
                 for eps in range(2):
                     src = pk[:, eps, :].rearrange("q (p u f) -> q u p f", u=2, f=2)
                     dst = kT[h][:, g, eps, :].rearrange("q (u p f) -> q u p f", u=2, f=2)
-                    if eps == 0:
+                    if g == 0:
                         nc.vector.tensor_copy(out=dst, in_=src)
                     else:
                         nc.scalar.copy(out=dst, in_=src)
@@ -348,10 +349,11 @@ def tile_hopfieldmemorylayer_pb_t_kernel(tc, q_scaled, k, v, norm_retrieved_w, q
                 tq(2, [0, 1, 2, 3])
             copy_q(it + 2)
             copy_e(it - 1)
+            if it == 1:
+                v_quant(0)
             negmax(it, 1)
             expo(it, 1)
             if it == 1:
-                v_quant(0)
                 v_quant(1)
             if it == 2:
                 nc.vector.tensor_scalar(out=w_bc[:], in0=w_bc[:], scalar1=32.0, scalar2=None, op0=ALU.mult)

from contextlib import ExitStack

import concourse.bass as bass
import concourse.mybir as mybir
import concourse.tile as tile
from concourse.masks import make_identity

F32 = mybir.dt.float32
BF16 = mybir.dt.bfloat16
U32 = mybir.dt.uint32
U8 = mybir.dt.uint8
FP8X4 = mybir.dt.float8_e4m3fn_x4
ACT = mybir.ActivationFunctionType
ALU = mybir.AluOpType
AX = mybir.AxisListType

P = 128
H = 2
D = 512
M = 512
E = H * D
R = 4096
TPC = 4
NCH = R // (P * TPC)
NT = R // P
EPS = 1e-6
FLOPS = 2 * R * M * D * H * 2

E_WORDS = True
PIN = True


def tile_hopfieldmemorylayer_pb_t_kernel(tc, q_scaled, k, v, norm_retrieved_w, query_input, out):
    nc = tc.nc
    qv = q_scaled.rearrange("b s h d -> (b s) (h d)").rearrange("(c p t) e -> c p t e", p=P, t=TPC)
    xv = query_input.rearrange("b s e -> (b s) e").rearrange("(c p t) e -> c p t e", p=P, t=TPC)
    ov = out.rearrange("b s e -> (b s) e").rearrange("(c p t) e -> c p t e", p=P, t=TPC)

    with ExitStack() as ctx:
        const = ctx.enter_context(tc.tile_pool(name="const", bufs=1))
        work = ctx.enter_context(tc.tile_pool(name="work", bufs=2))
        small = ctx.enter_context(tc.tile_pool(name="small", bufs=8))
        psum = ctx.enter_context(tc.psum_pool(name="psum", bufs=1))
        if PIN:
            ctx.enter_context(tc.manual_schedule())

        ident = const.tile([P, P], F32, name="ident")
        make_identity(nc, ident[:])
        ident_bf = const.tile([P, P], BF16, name="ident_bf")
        make_identity(nc, ident_bf[:])
        mhalf = const.tile([P, 1], F32, name="mhalf")
        nc.vector.memset(mhalf[:], -0.5)
        warm = const.tile([P, 1], F32, name="warm")
        wz = const.tile([P, M], BF16, name="wz")
        nc.vector.memset(wz[:], 0.0)
        nc.scalar.activation(out=warm[:], in_=mhalf[:], func=ACT.Exp)

        k_sb = [const.tile([P, 4, D], BF16, name="k_sb%d" % h) for h in range(H)]
        v_raw = [const.tile([P, 4, D], BF16, name="v_raw%d" % h) for h in range(H)]
        q_sb = [const.tile([P, TPC, E], BF16, name="q_sb%d" % c) for c in range(NCH)]
        x_sb = [const.tile([P, TPC, E], BF16, name="x_sb%d" % c) for c in range(NCH)]
        w_bc = const.tile([P, E], BF16, name="w_bc")
        nc.sync.dma_start(out=q_sb[0][:, 0:1, :], in_=qv[0][:, 0:1, :])
        for h in range(H):
            for a in (0, 2):
                nc.sync.dma_start(out=k_sb[h][:, a:a + 2, :], in_=k[h].rearrange("(a p) d -> p a d", p=P)[:, a:a + 2, :])
        nc.sync.dma_start(out=v_raw[0][:], in_=v[0].rearrange("(p j) w -> p j w", j=4))
        nc.sync.dma_start(out=q_sb[0][:, 1:2, :], in_=qv[0][:, 1:2, :])
        nc.sync.dma_start(out=q_sb[0][:, 2:3, :], in_=qv[0][:, 2:3, :])
        nc.sync.dma_start(out=v_raw[1][:], in_=v[1].rearrange("(p j) w -> p j w", j=4))
        nc.sync.dma_start(out=q_sb[0][:, 3:TPC, :], in_=qv[0][:, 3:TPC, :])
        nc.sync.dma_start(out=q_sb[1][:], in_=qv[1])
        nc.sync.dma_start(out=w_bc[:], in_=norm_retrieved_w.partition_broadcast(P))
        nc.sync.dma_start(out=x_sb[0][:], in_=xv[0])

        def load(c):
            if c + 2 < NCH:
                nc.sync.dma_start(out=q_sb[c + 2][:], in_=qv[c + 2])
            if c + 1 < NCH:
                nc.sync.dma_start(out=x_sb[c + 1][:], in_=xv[c + 1])

        kT = [const.tile([P, 2, 2, M], BF16, name="kT%d" % h) for h in range(H)]
        def kprep(h):
            pks = []
            for g in range(2):
                pk = psum.tile([P, 2, M], BF16, name="pk", tag=("acc0", "acc1", "acc1", "s")[2 * h + g], bufs=(1, 2, 2, 3)[2 * h + g])
                pks.append(pk)
            for a in range(4):
                for j in range(4):
                    nc.tensor.transpose(pks[j // 2][:, j % 2, a * P:(a + 1) * P], k_sb[h][:, a, j * P:(j + 1) * P], ident_bf[:])
            for g in range(2):
                pk = pks[g]
                for eps in range(2):
                    src = pk[:, eps, :].rearrange("q (p u f) -> q u p f", u=2, f=2)
                    dst = kT[h][:, g, eps, :].rearrange("q (u p f) -> q u p f", u=2, f=2)
                    if g == 0:
                        nc.vector.tensor_copy(out=dst, in_=src)
                    else:
                        nc.scalar.copy(out=dst, in_=src)

        v_codes = [const.tile([P, D], U32, name="v_codes%d" % h, align_bytes=256) for h in range(H)]
        v_scales = [const.tile([P, D], U8, name="v_scales%d" % h, align_bytes=256) for h in range(H)]
        v_grp = [const.tile([P, D, 4], BF16, name="v_grp%d" % h, align_bytes=256) for h in range(H)]

        def v_regroup(h):
            nc.gpsimd.tensor_scalar(out=v_grp[h][:], in0=v_raw[h][:].rearrange("p j w -> p w j"), scalar1=1.0, scalar2=0.0,
                                    op0=ALU.mult, op1=ALU.add)

        def v_quant(h):
            nc.vector.quantize_mx(out=v_codes[h][:].bitcast(FP8X4), scales=v_scales[h][:],
                                  in_=v_grp[h][:].rearrange("p w j -> p (w j)"))

        st = {}

        def ok(i):
            return 0 <= i < NT

        def tq(i, bs):
            if not ok(i):
                return
            c, t = divmod(i, TPC)
            if ("ptq", i) not in st:
                st[("ptq", i)] = psum.tile([P, 8 * P], BF16, name="ptq", tag="tq", bufs=1)
            for b in bs:
                for b2 in (2 * b, 2 * b + 1):
                    nc.tensor.transpose(st[("ptq", i)][:, b2 * P:(b2 + 1) * P], q_sb[c][:, t, b2 * P:(b2 + 1) * P], ident_bf[:])

        def copy_q(i):
            if not ok(i):
                return
            st[("qT", i)] = work.tile([P, 8 * P], BF16, name="qT", tag="qT", bufs=3)
            nc.scalar.copy(out=st[("qT", i)][:], in_=st[("ptq", i)][:])

        def mm(i, h, js):
            if not ok(i):
                return
            if ("s", i, h) not in st:
                st[("s", i, h)] = psum.tile([P, M], F32, name="ps_s", tag="s", bufs=3)
            qb = st[("qT", i)][:].rearrange("p (b r) -> p b r", b=8)
            for j in js:
                g, eps = divmod(j, 2)
                nc.tensor.matmul(out=st[("s", i, h)][:], lhsT=qb[:, 4 * h + j, :], rhs=kT[h][:, g, eps, :],
                                 start=(j == 0), stop=(j == 3))

        def mm_q(i):
            for j in range(4):
                mm(i, 0, [j])
                tq(i + 2, [j])

        def mm_e(i):
            mm(i, 1, [0])
            te(i - 1, 0, [0])
            mm(i, 1, [1])
            te(i - 1, 0, [1])
            mm(i, 1, [2])
            te(i - 1, 1, [0, 1])
            mm(i, 1, [3])

        def negmax(i, h):
            if not ok(i):
                return
            if h == 0:
                st[("nm", i)] = small.tile([P, H], F32, name="nm", tag="nm")
            nc.vector.tensor_reduce(out=st[("nm", i)][:, h:h + 1], in_=st[("s", i, h)][:], axis=AX.X, op=ALU.max, negate=True)

        def expo(i, h):
            if not ok(i):
                return
            if h == 0:
                st[("e", i)] = work.tile([P, H, M], BF16, name="e_sb", tag="e", bufs=3)
                st[("rs", i)] = small.tile([P, H], F32, name="rs", tag="rs")
            nc.scalar.activation(out=st[("e", i)][:, h, :], in_=st[("s", i, h)][:], func=ACT.Exp,
                                 bias=st[("nm", i)][:, h:h + 1], scale=1.0, accum_out=st[("rs", i)][:, h:h + 1])

        def recip(i):
            if not ok(i):
                return
            st[("inv", i)] = small.tile([P, H], F32, name="inv", tag="inv")
            nc.vector.reciprocal(out=st[("inv", i)][:], in_=st[("rs", i)][:])

        def te(i, h, us):
            if not ok(i):
                return
            if ("pte", i) not in st:
                if E_WORDS:
                    st[("pte", i)] = psum.tile([P, H, 2, P], F32, name="pte", tag="te", bufs=1)
                else:
                    st[("pte", i)] = psum.tile([P, H, 4, P], BF16, name="pte", tag="te", bufs=1)
            for u in us:
                if E_WORDS:
                    nc.tensor.transpose(st[("pte", i)][:, h, u, :], st[("e", i)][:, h, :].bitcast(F32)[:, u * P:(u + 1) * P], ident[:])
                else:
                    nc.tensor.transpose(st[("pte", i)][:, h, u, :], st[("e", i)][:, h, u * P:(u + 1) * P], ident_bf[:])

        def copy_e(i):
            if not ok(i):
                return
            if E_WORDS:
                st[("gq", i)] = work.tile([P, H, P, 2], F32, name="gq", tag="gq", bufs=3, align_bytes=256)
            else:
                st[("gq", i)] = work.tile([P, H, P, 4], BF16, name="gq", tag="gq", bufs=3, align_bytes=256)
            nc.scalar.copy(out=st[("gq", i)][:], in_=st[("pte", i)][:].rearrange("p h u r -> p h r u"))

        def quant(i):
            if not ok(i):
                return
            st[("cd", i)] = work.tile([P, H * P], U32, name="cd", tag="cd", bufs=2, align_bytes=256)
            st[("sc", i)] = work.tile([P, H * P], U8, name="sc", tag="sc", bufs=2, align_bytes=256)
            flat = st[("gq", i)][:].rearrange("p h r u -> p (h r u)")
            if E_WORDS:
                flat = flat.bitcast(BF16)
            nc.vector.quantize_mx(out=st[("cd", i)][:].bitcast(FP8X4), scales=st[("sc", i)][:], in_=flat)

        def mx(i):
            if not ok(i):
                return
            for h in range(H):
                if i == NT - 2:
                    st[("acc", i, h)] = psum.tile([P, D], F32, name="acc", tag="s", bufs=3)
                else:
                    st[("acc", i, h)] = psum.tile([P, D], F32, name="acc", tag=("acc0", "acc1")[h], bufs=(1, 2)[h])
                nc.tensor.matmul_mx(out=st[("acc", i, h)][:],
                                    lhsT=st[("cd", i)][:, h * P:(h + 1) * P].bitcast(FP8X4),
                                    lhsT_scale=st[("sc", i)][:, h * P:(h + 1) * P],
                                    rhs=v_codes[h][:].bitcast(FP8X4), rhs_scale=v_scales[h][:],
                                    start=True, stop=True)

        def sq(i, h):
            if not ok(i):
                return
            if ("ss", i) not in st:
                st[("ss", i)] = small.tile([P, H], F32, name="ss", tag="ss")
            junk = work.tile([P, D], BF16, name="junk", tag="junk", bufs=2)
            nc.scalar.activation(out=junk[:], in_=st[("acc", i, h)][:], func=ACT.Square,
                                 scale=st[("inv", i)][:, h:h + 1], accum_out=st[("ss", i)][:, h:h + 1])

        def zsum(i):
            if not ok(i):
                return
            st[("z", i)] = small.tile([P, 1], F32, name="z", tag="z")
            nc.vector.tensor_scalar(out=st[("z", i)][:], in0=st[("ss", i)][:, 0:1], scalar1=st[("ss", i)][:, 1:2], scalar2=E * EPS,
                                    op0=ALU.add, op1=ALU.add)

        def powr(i):
            if not ok(i):
                return
            st[("rr", i)] = small.tile([P, 1], F32, name="rr", tag="rr")
            nc.gpsimd.tensor_tensor(out=st[("rr", i)][:], in0=st[("z", i)][:], in1=mhalf[:], op=ALU.pow)

        def cmul(i):
            if not ok(i):
                return
            st[("c", i)] = small.tile([P, 1], F32, name="cc", tag="cc")
            nc.vector.tensor_scalar(out=st[("c", i)][:], in0=st[("inv", i)][:, 1:2], scalar1=st[("rr", i)][:, 0:1], scalar2=None, op0=ALU.mult)

        def scale0(i):
            if not ok(i):
                return
            st[("o", i)] = work.tile([P, E], F32, name="o_sb", tag="o", bufs=6)
            nc.vector.scalar_tensor_tensor(out=st[("o", i)][:, 0:D], in0=st[("acc", i, 0)][:], scalar=st[("inv", i)][:, 0:1],
                                           in1=w_bc[:, 0:D], op0=ALU.mult, op1=ALU.mult)

        def scale1(i):
            if not ok(i):
                return
            nc.vector.scalar_tensor_tensor(out=st[("o", i)][:, D:E], in0=st[("acc", i, 1)][:], scalar=st[("c", i)][:, 0:1],
                                           in1=w_bc[:, D:E], op0=ALU.mult, op1=ALU.mult)

        def scale1i(i):
            if not ok(i):
                return
            nc.vector.scalar_tensor_tensor(out=st[("o", i)][:, D:E], in0=st[("acc", i, 1)][:], scalar=st[("inv", i)][:, 1:2],
                                           in1=w_bc[:, D:E], op0=ALU.mult, op1=ALU.mult)

        def fin(i, lo, hi):
            c, t = divmod(i, TPC)
            nc.vector.scalar_tensor_tensor(out=st[("o", i)][:, lo:hi], in0=st[("o", i)][:, lo:hi], scalar=st[("rr", i)][:, 0:1],
                                           in1=x_sb[c][:, t, lo:hi], op0=ALU.mult, op1=ALU.add)

        def store_part(i, lo, hi):
            c, t = divmod(i, TPC)
            nc.sync.dma_start(out=ov[c][:, t, lo:hi], in_=st[("o", i)][:, lo:hi])

        def fin0(i):
            if not ok(i):
                return
            c, t = divmod(i, TPC)
            nc.vector.scalar_tensor_tensor(out=st[("o", i)][:, 0:D], in0=st[("o", i)][:, 0:D], scalar=st[("rr", i)][:, 0:1],
                                           in1=x_sb[c][:, t, 0:D], op0=ALU.mult, op1=ALU.add)

        def add_v(i):
            c, t = divmod(i, TPC)
            nc.vector.tensor_tensor(out=st[("o", i)][:, D:E], in0=st[("o", i)][:, D:E], in1=x_sb[c][:, t, D:E], op=ALU.add)

        def add_g(i):
            if not ok(i):
                return
            c, t = divmod(i, TPC)
            nc.gpsimd.tensor_tensor(out=st[("o", i)][:, D:E], in0=st[("o", i)][:, D:E], in1=x_sb[c][:, t, D:E], op=ALU.add)

        def store(i):
            if not ok(i):
                return
            c, t = divmod(i, TPC)
            nc.sync.dma_start(out=ov[c][:, t, :], in_=st[("o", i)][:])

        def warm_up(n):
            for rep in range(n):
                ps_w = psum.tile([P, M], F32, name="ps_w", tag="s", bufs=3)
                nc.tensor.matmul(out=ps_w[:], lhsT=wz[:, 0:P], rhs=wz[:], start=True, stop=True)

        v_regroup(0)
        v_regroup(1)
        warm_up(4)
        tq(0, [0, 1, 2, 3])
        copy_q(0)
        warm_up(1)
        kprep(0)
        warm_up(1)
        kprep(1)
        for it in range(NT):
            scale0(it - 3)
            cmul(it - 4)
            recip(it - 2)
            scale1(it - 4)
            if it == 0:
                mm(it, 0, [0, 1, 2, 3])
                tq(1, [0, 1, 2, 3])
                copy_q(1)
            elif it < 3:
                mm(it, 0, [0, 1, 2, 3])
                tq(it + 2, [0, 1, 2, 3])
            else:
                mm_q(it)
            sq(it - 3, 1)
            sq(it - 3, 0)
            negmax(it, 0)
            expo(it, 0)
            quant(it - 2)
            fin0(it - 4)
            zsum(it - 3)
            powr(it - 3)
            add_g(it - 4)
            store(it - 5)
            if it % TPC == 0:
                load(it // TPC)
            mm_e(it)
            if it == 0:
                tq(2, [0, 1, 2, 3])
            copy_q(it + 2)
            copy_e(it - 1)
            if it == 1:
                v_quant(0)
            negmax(it, 1)
            expo(it, 1)
            if it == 1:
                v_quant(1)
            if it == 2:
                nc.vector.tensor_scalar(out=w_bc[:], in0=w_bc[:], scalar1=32.0, scalar2=None, op0=ALU.mult)
            mx(it - 2)
        n = NT
        te(n - 1, 0, [0, 1])
        te(n - 1, 1, [0, 1])
        scale0(n - 3)
        cmul(n - 4)
        scale1i(n - 3)
        recip(n - 2)
        scale1(n - 4)
        sq(n - 3, 0)
        copy_e(n - 1)
        sq(n - 3, 1)
        quant(n - 2)
        mx(n - 2)
        store(n - 5)
        recip(n - 1)
        quant(n - 1)
        mx(n - 1)
        fin0(n - 4)
        zsum(n - 3)
        powr(n - 3)
        add_v(n - 4)
        store(n - 4)
        sq(n - 2, 0)
        sq(n - 2, 1)
        scale0(n - 2)
        scale1i(n - 2)
        zsum(n - 2)
        fin(n - 3, 0, D)
        store_part(n - 3, 0, D)
        powr(n - 2)
        sq(n - 1, 0)
        sq(n - 1, 1)
        scale0(n - 1)
        fin(n - 3, D, E)
        store_part(n - 3, D, E)
        zsum(n - 1)
        powr(n - 1)
        fin(n - 2, 0, D)
        store_part(n - 2, 0, D)
        scale1i(n - 1)
        fin(n - 2, D, E)
        store_part(n - 2, D, E)
        fin(n - 1, 0, D)
        store_part(n - 1, 0, D)
        for lo in (D, D + D // 2):
            fin(n - 1, lo, lo + D // 2)
            store_part(n - 1, lo, lo + D // 2)
